import numpy as np
import ml_dtypes


def mxq(x, axis, fmt="e4m3"):
    dtype, down = {"e4m3": (ml_dtypes.float8_e4m3fn, 7), "e5m2": (ml_dtypes.float8_e5m2, 14)}[fmt]
    v = np.moveaxis(np.asarray(x, np.float32).astype(ml_dtypes.bfloat16).astype(np.float64), axis, -1)
    blocks = v.reshape(v.shape[:-1] + (-1, 32))
    amax = np.abs(blocks).max(-1, keepdims=True)
    byte = np.maximum(np.where(amax > 0, np.frexp(amax)[1] - 1 + 127, 0) - down, 1)
    scale = np.exp2(byte - 127.0)
    codes = (blocks / scale).astype(np.float32).astype(dtype).astype(np.float64)
    return np.moveaxis((codes * scale).reshape(v.shape), -1, axis)


WIDE = False


def mx_kscale(k):
    if not WIDE:
        return np.ones(k)
    levels = np.array([10, -10, 5, -5, 0])
    a = np.random.permutation(np.resize(levels, k // 512 * 4)).reshape(k // 512, 4)
    idx = np.arange(k)
    return np.exp2(a[idx // 512, idx % 128 // 32])


BF16 = ml_dtypes.bfloat16


def bf(x):
    return np.asarray(x, np.float32).astype(BF16)


def f64(x):
    return np.asarray(x).astype(np.float64)


B, S, D, H, KVH, HD = 1, 512, 2048, 16, 4, 128
THETA = 10000.0


def rope(a, cos, sin):
    a1, a2 = a[..., 0::2], a[..., 1::2]
    c, s = cos[None, None], sin[None, None]
    return np.stack([a1 * c - a2 * s, a1 * s + a2 * c], axis=-1).reshape(a.shape)


def setup_inputs():
    s = mx_kscale(D)
    pos = np.arange(S) + np.random.randint(0, S)
    ang = np.outer(pos, 1.0 / THETA ** (np.arange(0, HD, 2) / HD))
    return {"x": bf(np.random.standard_normal((B, S, D)) * s),
            "cos": bf(np.cos(ang)), "sin": bf(np.sin(ang)),
            "Wq": bf(np.random.standard_normal((D, H * HD)) * 1.5 / np.sqrt(D) / s[:, None]),
            "Wkv": bf(np.random.standard_normal((D, 2 * KVH * HD)) * 1.5 / np.sqrt(D) / s[:, None])}


def reference(x, cos, sin, Wq, Wkv):
    xq = mxq(f64(x), 2, "e4m3")
    q = (xq @ mxq(f64(Wq), 0, "e4m3")).reshape(B, S, H, HD).transpose(0, 2, 1, 3)
    kv = (xq @ mxq(f64(Wkv), 0, "e4m3")).reshape(B, S, 2, KVH, HD)
    k = kv[:, :, 0].transpose(0, 2, 1, 3)
    v = kv[:, :, 1].transpose(0, 2, 1, 3)
    return rope(q, f64(cos), f64(sin)), rope(k, f64(cos), f64(sin)), v

@@ -1,0 +1,211 @@
+from contextlib import ExitStack
+
+import concourse.mybir as mybir
+from concourse.masks import make_identity
+
+FLOPS = 2 * 512 * 2048 * 3072
+
+BF16 = mybir.dt.bfloat16
+F32 = mybir.dt.float32
+U32 = mybir.dt.uint32
+U8 = mybir.dt.uint8
+FP8X4 = mybir.dt.float8_e4m3fn_x4
+MULT = mybir.AluOpType.mult
+ADD = mybir.AluOpType.add
+
+P = 128
+M = 4
+G = 4
+NB = 6
+NW = 512
+HD = 128
+HB = 4
+
+V_CHUNKS = ((0, 0), (0, 1), (0, 3))
+ADD_ON_GPSIMD = False
+MANUAL = False
+RAW_BUFS = 14
+
+
+def tile_gqa_pa_kernel(tc, x, cos, sin, Wq, Wkv, out_0, out_1, out_2):
+    nc = tc.nc
+    with ExitStack() as ctx:
+        const = ctx.enter_context(tc.tile_pool(name="const", bufs=1))
+        rawp = ctx.enter_context(tc.tile_pool(name="raw", bufs=RAW_BUFS))
+        wgp = ctx.enter_context(tc.tile_pool(name="wg", bufs=6))
+        wcp = ctx.enter_context(tc.tile_pool(name="wc", bufs=3))
+        zp = ctx.enter_context(tc.tile_pool(name="z", bufs=4))
+        op = ctx.enter_context(tc.tile_pool(name="o", bufs=3))
+        psum = ctx.enter_context(tc.psum_pool(name="psum", bufs=8))
+        if MANUAL:
+            ctx.enter_context(tc.manual_schedule())
+
+        xv = x.rearrange("b (p m) k -> p (b m) k", m=M)
+        cosv = cos.rearrange("(p m) i -> p m i", m=M)
+        sinv = sin.rearrange("(p m) i -> p m i", m=M)
+        outv = [o.rearrange("b h (p m) l -> p (b h) (m l)", m=M) for o in (out_0, out_1, out_2)]
+
+        def w_source(nb):
+            if nb < 4:
+                return Wq, nb * NW
+            return Wkv, (nb - 4) * NW
+
+        def out_dest(nb):
+            if nb < 4:
+                return outv[0][:, nb * HB:(nb + 1) * HB, :]
+            return outv[nb - 3][:, :, :]
+
+        cos_sb = const.tile([P, M, 64], BF16, name="cos_sb")
+        sin_sb = const.tile([P, M, 64], BF16, name="sin_sb")
+        nc.gpsimd.dma_start(out=cos_sb[:], in_=cosv)
+        nc.gpsimd.dma_start(out=sin_sb[:], in_=sinv)
+        ident = const.tile([P, P], F32, name="ident")
+        make_identity(nc, ident[:])
+
+        x_sb = const.tile([P, M, 2048], BF16, name="x_sb")
+        raw = {}
+
+        def load_x(m):
+            nc.sync.dma_start(out=x_sb[:, m, :], in_=xv[:, m, :])
+
+        def load_w(nb, g):
+            src, c0 = w_source(nb)
+            rw = rawp.tile([P, 4, NW], BF16, name="rw", tag="rw")
+            nc.sync.dma_start(
+                out=rw[:],
+                in_=src[g * 512:(g + 1) * 512, c0:c0 + NW].rearrange("(p j) n -> p j n", j=4),
+            )
+            raw[(nb, g)] = rw
+
+        load_x(0)
+        for g in range(G):
+            load_w(0, g)
+        for m in range(1, M):
+            load_x(m)
+        for nb in (1, 2):
+            for g in range(G):
+                load_w(nb, g)
+
+        tcomp = const.tile([P, M, 2, 64, 2], F32, name="tcomp")
+        nc.gpsimd.tensor_scalar(out=tcomp[:, :, 0, :, 0], in0=cos_sb[:], scalar1=1.0, scalar2=0.0, op0=MULT, op1=ADD)
+        nc.gpsimd.tensor_scalar(out=tcomp[:, :, 0, :, 1], in0=sin_sb[:], scalar1=1.0, scalar2=0.0, op0=MULT, op1=ADD)
+        nc.gpsimd.tensor_scalar(out=tcomp[:, :, 1, :, 0], in0=sin_sb[:], scalar1=-1.0, scalar2=0.0, op0=MULT, op1=ADD)
+        nc.gpsimd.tensor_scalar(out=tcomp[:, :, 1, :, 1], in0=cos_sb[:], scalar1=1.0, scalar2=0.0, op0=MULT, op1=ADD)
+        tab = const.tile([P, M, 2, HB, HD], F32, name="tab")
+        for m in range(M):
+            nc.gpsimd.tensor_scalar(
+                out=tab[:, m],
+                in0=tcomp[:, m].rearrange("p q i y -> p q (i y)").unsqueeze(2).to_broadcast([P, 2, HB, HD]),
+                scalar1=1.0, scalar2=0.0, op0=MULT, op1=ADD,
+            )
+
+        x32 = x_sb[:].bitcast(F32)
+        xg = const.tile([P, M, G, P, 4], BF16, name="xg", align_bytes=64)
+        xg32 = xg[:].bitcast(F32)
+        x_codes = const.tile([P, M, G, P], U32, name="x_codes", align_bytes=64)
+        x_scales = const.tile([P, M, G, P], U8, name="x_scales", align_bytes=64)
+
+        def prep_x(m):
+            words = x32[:, m, :].rearrange("p (g q u) -> p g u q", g=G, u=2)
+            for gh in range(2):
+                bank = psum.tile([P, 2, 2, P], F32, name="xt", tag="bank")
+                for gl in range(2):
+                    for u in range(2):
+                        nc.tensor.transpose(bank[:, gl, u, :], words[:, 2 * gh + gl, u, :], ident[:])
+                dst = xg32[:, m, 2 * gh:2 * gh + 2, :, :]
+                srcv = bank[:].rearrange("p g u s -> p g s u")
+                nc.scalar.copy(out=dst, in_=srcv)
+            nc.vector.quantize_mx(
+                out=x_codes[:, m].rearrange("p g s -> p (g s)").bitcast(FP8X4),
+                scales=x_scales[:, m].rearrange("p g s -> p (g s)"),
+                in_=xg[:, m].rearrange("p g s t -> p (g s t)"),
+            )
+
+        wq = {}
+
+        def stage1(nb):
+            wc = wcp.tile([P, G, NW], U32, name="wc", tag="wc", align_bytes=64)
+            ws = wcp.tile([P, G, NW], U8, name="ws", tag="ws", align_bytes=64)
+            wq[nb] = (wc, ws)
+            tiles = []
+            for g in range(G):
+                wg = wgp.tile([P, NW, 4], BF16, name="wg", tag="wg", align_bytes=64)
+                dst = wg[:].rearrange("p (c i) t -> p c t i", i=4)
+                srcv = raw[(nb, g)][:].rearrange("p t (c i) -> p c t i", i=4)
+                if (nb, g) in V_CHUNKS:
+                    nc.vector.tensor_copy(out=dst, in_=srcv)
+                else:
+                    nc.scalar.copy(out=dst, in_=srcv)
+                tiles.append(wg)
+            for g in range(G):
+                nc.vector.quantize_mx(
+                    out=wc[:, g, :].bitcast(FP8X4),
+                    scales=ws[:, g, :],
+                    in_=tiles[g][:].rearrange("p n t -> p (n t)"),
+                )
+
+        acc = {}
+
+        def mx_pass(nb, m, g):
+            wc, ws = wq[nb]
+            nc.tensor.matmul_mx(
+                out=acc[(nb, m)][:],
+                lhsT=x_codes[:, m, g, :].bitcast(FP8X4),
+                lhsT_scale=x_scales[:, m, g, :],
+                rhs=wc[:, g, :].bitcast(FP8X4),
+                rhs_scale=ws[:, g, :],
+                start=(g == 0),
+                stop=(g == G - 1),
+            )
+
+        def mx(nb, m_outer):
+            for m in range(M):
+                acc[(nb, m)] = psum.tile([P, NW], F32, name="acc", tag="bank")
+            if m_outer:
+                for m in range(M):
+                    for g in range(G):
+                        mx_pass(nb, m, g)
+            else:
+                for g in range(G):
+                    for m in range(M):
+                        mx_pass(nb, m, g)
+
+        def finish(nb):
+            ost = op.tile([P, HB, M, HD], F32, name="ost", tag="ost")
+            for m in range(M):
+                a = acc[(nb, m)]
+                if nb == NB - 1:
+                    av = a[:].rearrange("p (h l) -> p h l", h=HB)
+                    if m % 2 == 0:
+                        nc.scalar.copy(out=ost[:, :, m, :], in_=av)
+                    else:
+                        nc.vector.tensor_copy(out=ost[:, :, m, :], in_=av)
+                    continue
+                z = zp.tile([P, 2, HB * 64, 2], F32, name="z", tag="z")
+                nc.vector.tensor_tensor(
+                    out=z[:],
+                    in0=a[:].rearrange("p (c q) -> p q c", q=2).unsqueeze(3).to_broadcast([P, 2, HB * 64, 2]),
+                    in1=tab[:, m].rearrange("p q h (i y) -> p q (h i) y", y=2),
+                    op=MULT,
+                )
+                eng = nc.gpsimd if ADD_ON_GPSIMD else nc.vector
+                eng.tensor_tensor(
+                    out=ost[:, :, m, :],
+                    in0=z[:, 0].rearrange("p (h i) y -> p h (i y)", h=HB),
+                    in1=z[:, 1].rearrange("p (h i) y -> p h (i y)", h=HB),
+                    op=ADD,
+                )
+            nc.sync.dma_start(out=out_dest(nb), in_=ost[:].rearrange("p h m l -> p h (m l)"))
+
+        prep_x(0)
+        stage1(0)
+        for m in range(1, M):
+            prep_x(m)
+        for nb in range(NB):
+            mx(nb, m_outer=(nb == 0))
+            if nb + 1 < NB:
+                stage1(nb + 1)
+            if nb + 3 < NB:
+                for g in range(G):
+                    load_w(nb + 3, g)
+            finish(nb)

@@ -21,8 +21,8 @@ NW = 512
 HD = 128
 HB = 4
 
-V_CHUNKS = ((0, 0), (0, 1), (0, 3))
-ADD_ON_GPSIMD = False
+V_CHUNKS = ((0, 0), (0, 1), (0, 3), (1, 2), (2, 2), (3, 2))
+ADD_ON_GPSIMD = True
 MANUAL = False
 RAW_BUFS = 14
 

@@ -21,10 +21,16 @@ NW = 512
 HD = 128
 HB = 4
 
-V_CHUNKS = ((0, 0), (0, 1), (0, 3), (1, 2), (2, 2), (3, 2))
-ADD_ON_GPSIMD = True
-MANUAL = False
-RAW_BUFS = 14
+PATHS = (("V", "V", "S", "V"), ("S", "PS", "V", "PS"), ("S", "PS", "V", "PS"), ("S", "PS", "V", "PS"), ("S", "PS", "S", "PS"), ("S", "PS", "S", "S"))
+ADD_V = ()
+M_OUTER = (0, 1, 2, 3, 4)
+LEAD = 2
+RAW_BUFS = 16
+LOAD_LEAD = 4
+WG_BUFS = 8
+ACC_BUFS = 4
+AUX_BUFS = 4
+V_COPY = ("S", "V", "S", "V")
 
 
 def tile_gqa_pa_kernel(tc, x, cos, sin, Wq, Wkv, out_0, out_1, out_2):
@@ -32,13 +38,12 @@ def tile_gqa_pa_kernel(tc, x, cos, sin, Wq, Wkv, out_0, out_1, out_2):
     with ExitStack() as ctx:
         const = ctx.enter_context(tc.tile_pool(name="const", bufs=1))
         rawp = ctx.enter_context(tc.tile_pool(name="raw", bufs=RAW_BUFS))
-        wgp = ctx.enter_context(tc.tile_pool(name="wg", bufs=6))
+        wgp = ctx.enter_context(tc.tile_pool(name="wg", bufs=WG_BUFS))
         wcp = ctx.enter_context(tc.tile_pool(name="wc", bufs=3))
         zp = ctx.enter_context(tc.tile_pool(name="z", bufs=4))
         op = ctx.enter_context(tc.tile_pool(name="o", bufs=3))
-        psum = ctx.enter_context(tc.psum_pool(name="psum", bufs=8))
-        if MANUAL:
-            ctx.enter_context(tc.manual_schedule())
+        accp = ctx.enter_context(tc.psum_pool(name="accp", bufs=ACC_BUFS))
+        auxp = ctx.enter_context(tc.psum_pool(name="auxp", bufs=AUX_BUFS))
 
         xv = x.rearrange("b (p m) k -> p (b m) k", m=M)
         cosv = cos.rearrange("(p m) i -> p m i", m=M)
@@ -61,6 +66,8 @@ def tile_gqa_pa_kernel(tc, x, cos, sin, Wq, Wkv, out_0, out_1, out_2):
         nc.gpsimd.dma_start(out=sin_sb[:], in_=sinv)
         ident = const.tile([P, P], F32, name="ident")
         make_identity(nc, ident[:])
+        identb = const.tile([P, P], BF16, name="identb")
+        make_identity(nc, identb[:])
 
         x_sb = const.tile([P, M, 2048], BF16, name="x_sb")
         raw = {}
@@ -82,7 +89,7 @@ def tile_gqa_pa_kernel(tc, x, cos, sin, Wq, Wkv, out_0, out_1, out_2):
             load_w(0, g)
         for m in range(1, M):
             load_x(m)
-        for nb in (1, 2):
+        for nb in range(1, LOAD_LEAD):
             for g in range(G):
                 load_w(nb, g)
 
@@ -108,7 +115,7 @@ def tile_gqa_pa_kernel(tc, x, cos, sin, Wq, Wkv, out_0, out_1, out_2):
         def prep_x(m):
             words = x32[:, m, :].rearrange("p (g q u) -> p g u q", g=G, u=2)
             for gh in range(2):
-                bank = psum.tile([P, 2, 2, P], F32, name="xt", tag="bank")
+                bank = auxp.tile([P, 2, 2, P], F32, name="xt", tag="aux")
                 for gl in range(2):
                     for u in range(2):
                         nc.tensor.transpose(bank[:, gl, u, :], words[:, 2 * gh + gl, u, :], ident[:])
@@ -122,26 +129,47 @@ def tile_gqa_pa_kernel(tc, x, cos, sin, Wq, Wkv, out_0, out_1, out_2):
             )
 
         wq = {}
+        wgs = {}
 
-        def stage1(nb):
+        def regroup(nb):
+            for g in range(G):
+                path = PATHS[nb][g]
+                wg = wgp.tile([P, NW, 4], BF16, name="wg", tag="wg", align_bytes=64)
+                wgs[(nb, g)] = wg
+                dst = wg[:].rearrange("p (c i) t -> p c t i", i=4)
+                srcv = raw[(nb, g)][:].rearrange("p t (c i) -> p c t i", i=4)
+                if path == "V":
+                    nc.vector.tensor_copy(out=dst, in_=srcv)
+                elif path == "S":
+                    nc.scalar.copy(out=dst, in_=srcv)
+                else:
+                    flat = wg[:].rearrange("p n t -> p (n t)")
+                    for half in range(2):
+                        wi = auxp.tile([P, 2, P, 4], BF16, name="wi", tag="aux")
+                        for q in range(2):
+                            c0 = (2 * half + q) * P
+                            nc.tensor.matmul(
+                                out=wi[:, q],
+                                lhsT=identb[:],
+                                rhs=raw[(nb, g)][:, :, c0:c0 + P].rearrange("p t c -> p c t"),
+                                start=True, stop=True,
+                            )
+                        o_ = flat[:, half * 1024:(half + 1) * 1024]
+                        i_ = wi[:].rearrange("p q c t -> p (q c t)")
+                        if path == "PS":
+                            nc.scalar.copy(out=o_, in_=i_)
+                        else:
+                            nc.vector.tensor_copy(out=o_, in_=i_)
+
+        def quant(nb):
             wc = wcp.tile([P, G, NW], U32, name="wc", tag="wc", align_bytes=64)
             ws = wcp.tile([P, G, NW], U8, name="ws", tag="ws", align_bytes=64)
             wq[nb] = (wc, ws)
-            tiles = []
-            for g in range(G):
-                wg = wgp.tile([P, NW, 4], BF16, name="wg", tag="wg", align_bytes=64)
-                dst = wg[:].rearrange("p (c i) t -> p c t i", i=4)
-                srcv = raw[(nb, g)][:].rearrange("p t (c i) -> p c t i", i=4)
-                if (nb, g) in V_CHUNKS:
-                    nc.vector.tensor_copy(out=dst, in_=srcv)
-                else:
-                    nc.scalar.copy(out=dst, in_=srcv)
-                tiles.append(wg)
             for g in range(G):
                 nc.vector.quantize_mx(
                     out=wc[:, g, :].bitcast(FP8X4),
                     scales=ws[:, g, :],
-                    in_=tiles[g][:].rearrange("p n t -> p (n t)"),
+                    in_=wgs[(nb, g)][:].rearrange("p n t -> p (n t)"),
                 )
 
         acc = {}
@@ -159,53 +187,70 @@ def tile_gqa_pa_kernel(tc, x, cos, sin, Wq, Wkv, out_0, out_1, out_2):
             )
 
         def mx(nb, m_outer):
-            for m in range(M):
-                acc[(nb, m)] = psum.tile([P, NW], F32, name="acc", tag="bank")
             if m_outer:
                 for m in range(M):
+                    acc[(nb, m)] = accp.tile([P, NW], F32, name="acc", tag="acc")
                     for g in range(G):
                         mx_pass(nb, m, g)
             else:
+                for m in range(M):
+                    acc[(nb, m)] = accp.tile([P, NW], F32, name="acc", tag="acc")
                 for g in range(G):
                     for m in range(M):
                         mx_pass(nb, m, g)
 
         def finish(nb):
             ost = op.tile([P, HB, M, HD], F32, name="ost", tag="ost")
+            zs = {}
             for m in range(M):
                 a = acc[(nb, m)]
                 if nb == NB - 1:
                     av = a[:].rearrange("p (h l) -> p h l", h=HB)
-                    if m % 2 == 0:
+                    if V_COPY[m] == "S":
                         nc.scalar.copy(out=ost[:, :, m, :], in_=av)
                     else:
                         nc.vector.tensor_copy(out=ost[:, :, m, :], in_=av)
                     continue
                 z = zp.tile([P, 2, HB * 64, 2], F32, name="z", tag="z")
+                zs[m] = z
                 nc.vector.tensor_tensor(
                     out=z[:],
                     in0=a[:].rearrange("p (c q) -> p q c", q=2).unsqueeze(3).to_broadcast([P, 2, HB * 64, 2]),
                     in1=tab[:, m].rearrange("p q h (i y) -> p q (h i) y", y=2),
                     op=MULT,
                 )
-                eng = nc.gpsimd if ADD_ON_GPSIMD else nc.vector
-                eng.tensor_tensor(
-                    out=ost[:, :, m, :],
-                    in0=z[:, 0].rearrange("p (h i) y -> p h (i y)", h=HB),
-                    in1=z[:, 1].rearrange("p (h i) y -> p h (i y)", h=HB),
-                    op=ADD,
-                )
+                if m not in ADD_V:
+                    nc.gpsimd.tensor_tensor(
+                        out=ost[:, :, m, :],
+                        in0=z[:, 0].rearrange("p (h i) y -> p h (i y)", h=HB),
+                        in1=z[:, 1].rearrange("p (h i) y -> p h (i y)", h=HB),
+                        op=ADD,
+                    )
+            for m in sorted(zs):
+                if m in ADD_V:
+                    z = zs[m]
+                    nc.vector.tensor_tensor(
+                        out=ost[:, :, m, :],
+                        in0=z[:, 0].rearrange("p (h i) y -> p h (i y)", h=HB),
+                        in1=z[:, 1].rearrange("p (h i) y -> p h (i y)", h=HB),
+                        op=ADD,
+                    )
             nc.sync.dma_start(out=out_dest(nb), in_=ost[:].rearrange("p h m l -> p h (m l)"))
 
         prep_x(0)
-        stage1(0)
+        regroup(0)
+        quant(0)
         for m in range(1, M):
             prep_x(m)
+        for nb in range(1, LEAD):
+            regroup(nb)
         for nb in range(NB):
-            mx(nb, m_outer=(nb == 0))
+            if nb + LEAD < NB:
+                regroup(nb + LEAD)
             if nb + 1 < NB:
-                stage1(nb + 1)
-            if nb + 3 < NB:
+                quant(nb + 1)
+            mx(nb, m_outer=(nb in M_OUTER))
+            if nb + LOAD_LEAD < NB:
                 for g in range(G):
-                    load_w(nb + 3, g)
+                    load_w(nb + LOAD_LEAD, g)
             finish(nb)

@@ -21,7 +21,7 @@ NW = 512
 HD = 128
 HB = 4
 
-PATHS = (("V", "V", "S", "V"), ("S", "PS", "V", "PS"), ("S", "PS", "V", "PS"), ("S", "PS", "V", "PS"), ("S", "PS", "S", "PS"), ("S", "PS", "S", "S"))
+PATHS = (("V", "V", "S", "V"), ("S", "S", "V", "S"), ("S", "S", "V", "S"), ("S", "S", "V", "S"), ("S", "S", "S", "S"), ("S", "S", "S", "S"))
 ADD_V = ()
 M_OUTER = (0, 1, 2, 3, 4)
 LEAD = 2

@@ -22,7 +22,7 @@ HD = 128
 HB = 4
 
 PATHS = (("V", "V", "S", "V"), ("S", "S", "V", "S"), ("S", "S", "V", "S"), ("S", "S", "V", "S"), ("S", "S", "S", "S"), ("S", "S", "S", "S"))
-ADD_V = ()
+ADD_V = (2, 3)
 M_OUTER = (0, 1, 2, 3, 4)
 LEAD = 2
 RAW_BUFS = 16

@@ -21,16 +21,19 @@ NW = 512
 HD = 128
 HB = 4
 
-PATHS = (("V", "V", "S", "V"), ("S", "S", "V", "S"), ("S", "S", "V", "S"), ("S", "S", "V", "S"), ("S", "S", "S", "S"), ("S", "S", "S", "S"))
+PATHS = (("V", "V", "S", "V"), ("S", "S", "V", "S"), ("S", "S", "V", "S"), ("S", "S", "V", "S"), ("S", "S", "V", "S"), ("S", "S", "S", "S"))
 ADD_V = (2, 3)
 M_OUTER = (0, 1, 2, 3, 4)
 LEAD = 2
 RAW_BUFS = 16
 LOAD_LEAD = 4
-WG_BUFS = 8
-ACC_BUFS = 4
-AUX_BUFS = 4
-V_COPY = ("S", "V", "S", "V")
+WG_BUFS = 4
+QW = 2
+ACC_BUFS = 8
+AUX_BUFS = 0
+V_COPY = ("S", "S", "S", "S")
+ORDER = (0, 1, 2, 3, 4, 5)
+PARTS_FROM = 4
 
 
 def tile_gqa_pa_kernel(tc, x, cos, sin, Wq, Wkv, out_0, out_1, out_2):
@@ -43,7 +46,8 @@ def tile_gqa_pa_kernel(tc, x, cos, sin, Wq, Wkv, out_0, out_1, out_2):
         zp = ctx.enter_context(tc.tile_pool(name="z", bufs=4))
         op = ctx.enter_context(tc.tile_pool(name="o", bufs=3))
         accp = ctx.enter_context(tc.psum_pool(name="accp", bufs=ACC_BUFS))
-        auxp = ctx.enter_context(tc.psum_pool(name="auxp", bufs=AUX_BUFS))
+        auxp = ctx.enter_context(tc.psum_pool(name="auxp", bufs=AUX_BUFS)) if AUX_BUFS else accp
+        aux_tag = "aux" if AUX_BUFS else "acc"
 
         xv = x.rearrange("b (p m) k -> p (b m) k", m=M)
         cosv = cos.rearrange("(p m) i -> p m i", m=M)
@@ -86,12 +90,12 @@ def tile_gqa_pa_kernel(tc, x, cos, sin, Wq, Wkv, out_0, out_1, out_2):
 
         load_x(0)
         for g in range(G):
-            load_w(0, g)
+            load_w(ORDER[0], g)
         for m in range(1, M):
             load_x(m)
-        for nb in range(1, LOAD_LEAD):
+        for i in range(1, LOAD_LEAD):
             for g in range(G):
-                load_w(nb, g)
+                load_w(ORDER[i], g)
 
         tcomp = const.tile([P, M, 2, 64, 2], F32, name="tcomp")
         nc.gpsimd.tensor_scalar(out=tcomp[:, :, 0, :, 0], in0=cos_sb[:], scalar1=1.0, scalar2=0.0, op0=MULT, op1=ADD)
@@ -115,7 +119,7 @@ def tile_gqa_pa_kernel(tc, x, cos, sin, Wq, Wkv, out_0, out_1, out_2):
         def prep_x(m):
             words = x32[:, m, :].rearrange("p (g q u) -> p g u q", g=G, u=2)
             for gh in range(2):
-                bank = auxp.tile([P, 2, 2, P], F32, name="xt", tag="aux")
+                bank = auxp.tile([P, 2, 2, P], F32, name="xt", tag=aux_tag)
                 for gl in range(2):
                     for u in range(2):
                         nc.tensor.transpose(bank[:, gl, u, :], words[:, 2 * gh + gl, u, :], ident[:])
@@ -133,19 +137,21 @@ def tile_gqa_pa_kernel(tc, x, cos, sin, Wq, Wkv, out_0, out_1, out_2):
 
         def regroup(nb):
             for g in range(G):
-                path = PATHS[nb][g]
-                wg = wgp.tile([P, NW, 4], BF16, name="wg", tag="wg", align_bytes=64)
-                wgs[(nb, g)] = wg
-                dst = wg[:].rearrange("p (c i) t -> p c t i", i=4)
+                path = PATHS[ORDER.index(nb)][g]
+                if g % QW == 0:
+                    wgt = wgp.tile([P, QW, NW, 4], BF16, name="wgt", tag="wg", align_bytes=64)
+                    wgs[(nb, g // QW)] = wgt
+                wg = wgs[(nb, g // QW)][:, g % QW]
+                dst = wg.rearrange("p (c i) t -> p c t i", i=4)
                 srcv = raw[(nb, g)][:].rearrange("p t (c i) -> p c t i", i=4)
                 if path == "V":
                     nc.vector.tensor_copy(out=dst, in_=srcv)
                 elif path == "S":
                     nc.scalar.copy(out=dst, in_=srcv)
                 else:
-                    flat = wg[:].rearrange("p n t -> p (n t)")
+                    flat = wg.rearrange("p n t -> p (n t)")
                     for half in range(2):
-                        wi = auxp.tile([P, 2, P, 4], BF16, name="wi", tag="aux")
+                        wi = auxp.tile([P, 2, P, 4], BF16, name="wi", tag=aux_tag)
                         for q in range(2):
                             c0 = (2 * half + q) * P
                             nc.tensor.matmul(
@@ -165,11 +171,11 @@ def tile_gqa_pa_kernel(tc, x, cos, sin, Wq, Wkv, out_0, out_1, out_2):
             wc = wcp.tile([P, G, NW], U32, name="wc", tag="wc", align_bytes=64)
             ws = wcp.tile([P, G, NW], U8, name="ws", tag="ws", align_bytes=64)
             wq[nb] = (wc, ws)
-            for g in range(G):
+            for h in range(G // QW):
                 nc.vector.quantize_mx(
-                    out=wc[:, g, :].bitcast(FP8X4),
-                    scales=ws[:, g, :],
-                    in_=wgs[(nb, g)][:].rearrange("p n t -> p (n t)"),
+                    out=wc[:, h * QW:(h + 1) * QW, :].rearrange("p g n -> p (g n)").bitcast(FP8X4),
+                    scales=ws[:, h * QW:(h + 1) * QW, :].rearrange("p g n -> p (g n)"),
+                    in_=wgs[(nb, h)][:].rearrange("p g n t -> p (g n t)"),
                 )
 
         acc = {}
@@ -201,6 +207,21 @@ def tile_gqa_pa_kernel(tc, x, cos, sin, Wq, Wkv, out_0, out_1, out_2):
 
         def finish(nb):
             ost = op.tile([P, HB, M, HD], F32, name="ost", tag="ost")
+            parts = ORDER.index(nb) >= PARTS_FROM
+
+            def done(m):
+                if parts:
+                    nc.sync.dma_start(out=out_dest(nb)[:, :, m * HD:(m + 1) * HD], in_=ost[:, :, m, :])
+
+            def add(eng, m, z):
+                eng.tensor_tensor(
+                    out=ost[:, :, m, :],
+                    in0=z[:, 0].rearrange("p (h i) y -> p h (i y)", h=HB),
+                    in1=z[:, 1].rearrange("p (h i) y -> p h (i y)", h=HB),
+                    op=ADD,
+                )
+                done(m)
+
             zs = {}
             for m in range(M):
                 a = acc[(nb, m)]
@@ -210,6 +231,7 @@ def tile_gqa_pa_kernel(tc, x, cos, sin, Wq, Wkv, out_0, out_1, out_2):
                         nc.scalar.copy(out=ost[:, :, m, :], in_=av)
                     else:
                         nc.vector.tensor_copy(out=ost[:, :, m, :], in_=av)
+                    done(m)
                     continue
                 z = zp.tile([P, 2, HB * 64, 2], F32, name="z", tag="z")
                 zs[m] = z
@@ -220,37 +242,27 @@ def tile_gqa_pa_kernel(tc, x, cos, sin, Wq, Wkv, out_0, out_1, out_2):
                     op=MULT,
                 )
                 if m not in ADD_V:
-                    nc.gpsimd.tensor_tensor(
-                        out=ost[:, :, m, :],
-                        in0=z[:, 0].rearrange("p (h i) y -> p h (i y)", h=HB),
-                        in1=z[:, 1].rearrange("p (h i) y -> p h (i y)", h=HB),
-                        op=ADD,
-                    )
+                    add(nc.gpsimd, m, z)
             for m in sorted(zs):
                 if m in ADD_V:
-                    z = zs[m]
-                    nc.vector.tensor_tensor(
-                        out=ost[:, :, m, :],
-                        in0=z[:, 0].rearrange("p (h i) y -> p h (i y)", h=HB),
-                        in1=z[:, 1].rearrange("p (h i) y -> p h (i y)", h=HB),
-                        op=ADD,
-                    )
-            nc.sync.dma_start(out=out_dest(nb), in_=ost[:].rearrange("p h m l -> p h (m l)"))
+                    add(nc.vector, m, zs[m])
+            if not parts:
+                nc.sync.dma_start(out=out_dest(nb), in_=ost[:].rearrange("p h m l -> p h (m l)"))
 
         prep_x(0)
-        regroup(0)
-        quant(0)
+        regroup(ORDER[0])
+        quant(ORDER[0])
         for m in range(1, M):
             prep_x(m)
-        for nb in range(1, LEAD):
-            regroup(nb)
-        for nb in range(NB):
-            if nb + LEAD < NB:
-                regroup(nb + LEAD)
-            if nb + 1 < NB:
-                quant(nb + 1)
-            mx(nb, m_outer=(nb in M_OUTER))
-            if nb + LOAD_LEAD < NB:
+        for i in range(1, LEAD):
+            regroup(ORDER[i])
+        for i in range(NB):
+            if i + LEAD < NB:
+                regroup(ORDER[i + LEAD])
+            if i + 1 < NB:
+                quant(ORDER[i + 1])
+            mx(ORDER[i], m_outer=(i in M_OUTER))
+            if i + LOAD_LEAD < NB:
                 for g in range(G):
-                    load_w(nb + LOAD_LEAD, g)
-            finish(nb)
+                    load_w(ORDER[i + LOAD_LEAD], g)
+            finish(ORDER[i])

@@ -22,10 +22,12 @@ HD = 128
 HB = 4
 
 PATHS = (("V", "V", "S", "V"), ("S", "S", "V", "S"), ("S", "S", "V", "S"), ("S", "S", "V", "S"), ("S", "S", "V", "S"), ("S", "S", "S", "S"))
-ADD_V = (2, 3)
+ADD_V = ((2, 3), (2, 3), (2, 3), (2, 3), (2, 3), ())
 M_OUTER = (0, 1, 2, 3, 4)
 LEAD = 2
-RAW_BUFS = 16
+RAW_BUFS = 8
+PAIR_FROM = 2
+RAW2_BUFS = 6
 LOAD_LEAD = 4
 WG_BUFS = 4
 QW = 2
@@ -41,6 +43,7 @@ def tile_gqa_pa_kernel(tc, x, cos, sin, Wq, Wkv, out_0, out_1, out_2):
     with ExitStack() as ctx:
         const = ctx.enter_context(tc.tile_pool(name="const", bufs=1))
         rawp = ctx.enter_context(tc.tile_pool(name="raw", bufs=RAW_BUFS))
+        raw2p = ctx.enter_context(tc.tile_pool(name="raw2", bufs=RAW2_BUFS))
         wgp = ctx.enter_context(tc.tile_pool(name="wg", bufs=WG_BUFS))
         wcp = ctx.enter_context(tc.tile_pool(name="wc", bufs=3))
         zp = ctx.enter_context(tc.tile_pool(name="z", bufs=4))
@@ -73,20 +76,34 @@ def tile_gqa_pa_kernel(tc, x, cos, sin, Wq, Wkv, out_0, out_1, out_2):
         identb = const.tile([P, P], BF16, name="identb")
         make_identity(nc, identb[:])
 
-        x_sb = const.tile([P, M, 2048], BF16, name="x_sb")
+        x_sb = {}
         raw = {}
 
         def load_x(m):
-            nc.sync.dma_start(out=x_sb[:, m, :], in_=xv[:, m, :])
+            x_sb[m] = rawp.tile([P, 2048], BF16, name="xs", tag="rw")
+            nc.sync.dma_start(out=x_sb[m][:], in_=xv[:, m, :])
 
         def load_w(nb, g):
             src, c0 = w_source(nb)
+            place = ORDER.index(nb)
+            if place >= PAIR_FROM:
+                if (place - PAIR_FROM) % 2 == 1:
+                    return
+                assert ORDER[place + 1] == nb + 1
+                rw2 = raw2p.tile([P, 4, 2 * NW], BF16, name="rw2", tag="rw2")
+                nc.sync.dma_start(
+                    out=rw2[:],
+                    in_=src[g * 512:(g + 1) * 512, c0:c0 + 2 * NW].rearrange("(p j) n -> p j n", j=4),
+                )
+                raw[(nb, g)] = rw2[:, :, 0:NW]
+                raw[(nb + 1, g)] = rw2[:, :, NW:2 * NW]
+                return
             rw = rawp.tile([P, 4, NW], BF16, name="rw", tag="rw")
             nc.sync.dma_start(
                 out=rw[:],
                 in_=src[g * 512:(g + 1) * 512, c0:c0 + NW].rearrange("(p j) n -> p j n", j=4),
             )
-            raw[(nb, g)] = rw
+            raw[(nb, g)] = rw[:]
 
         load_x(0)
         for g in range(G):
@@ -110,14 +127,13 @@ def tile_gqa_pa_kernel(tc, x, cos, sin, Wq, Wkv, out_0, out_1, out_2):
                 scalar1=1.0, scalar2=0.0, op0=MULT, op1=ADD,
             )
 
-        x32 = x_sb[:].bitcast(F32)
         xg = const.tile([P, M, G, P, 4], BF16, name="xg", align_bytes=64)
         xg32 = xg[:].bitcast(F32)
         x_codes = const.tile([P, M, G, P], U32, name="x_codes", align_bytes=64)
         x_scales = const.tile([P, M, G, P], U8, name="x_scales", align_bytes=64)
 
         def prep_x(m):
-            words = x32[:, m, :].rearrange("p (g q u) -> p g u q", g=G, u=2)
+            words = x_sb[m][:].bitcast(F32).rearrange("p (g q u) -> p g u q", g=G, u=2)
             for gh in range(2):
                 bank = auxp.tile([P, 2, 2, P], F32, name="xt", tag=aux_tag)
                 for gl in range(2):
@@ -134,6 +150,7 @@ def tile_gqa_pa_kernel(tc, x, cos, sin, Wq, Wkv, out_0, out_1, out_2):
 
         wq = {}
         wgs = {}
+        pending = []
 
         def regroup(nb):
             for g in range(G):
@@ -143,7 +160,7 @@ def tile_gqa_pa_kernel(tc, x, cos, sin, Wq, Wkv, out_0, out_1, out_2):
                     wgs[(nb, g // QW)] = wgt
                 wg = wgs[(nb, g // QW)][:, g % QW]
                 dst = wg.rearrange("p (c i) t -> p c t i", i=4)
-                srcv = raw[(nb, g)][:].rearrange("p t (c i) -> p c t i", i=4)
+                srcv = raw[(nb, g)].rearrange("p t (c i) -> p c t i", i=4)
                 if path == "V":
                     nc.vector.tensor_copy(out=dst, in_=srcv)
                 elif path == "S":
@@ -165,7 +182,7 @@ def tile_gqa_pa_kernel(tc, x, cos, sin, Wq, Wkv, out_0, out_1, out_2):
                         if path == "PS":
                             nc.scalar.copy(out=o_, in_=i_)
                         else:
-                            nc.vector.tensor_copy(out=o_, in_=i_)
+                            pending.append((o_, i_))
 
         def quant(nb):
             wc = wcp.tile([P, G, NW], U32, name="wc", tag="wc", align_bytes=64)
@@ -208,6 +225,7 @@ def tile_gqa_pa_kernel(tc, x, cos, sin, Wq, Wkv, out_0, out_1, out_2):
         def finish(nb):
             ost = op.tile([P, HB, M, HD], F32, name="ost", tag="ost")
             parts = ORDER.index(nb) >= PARTS_FROM
+            add_v = ADD_V[ORDER.index(nb)]
 
             def done(m):
                 if parts:
@@ -241,10 +259,13 @@ def tile_gqa_pa_kernel(tc, x, cos, sin, Wq, Wkv, out_0, out_1, out_2):
                     in1=tab[:, m].rearrange("p q h (i y) -> p q (h i) y", y=2),
                     op=MULT,
                 )
-                if m not in ADD_V:
+                if m not in add_v:
                     add(nc.gpsimd, m, z)
+            for o_, i_ in pending:
+                nc.vector.tensor_copy(out=o_, in_=i_)
+            pending.clear()
             for m in sorted(zs):
-                if m in ADD_V:
+                if m in add_v:
                     add(nc.vector, m, zs[m])
             if not parts:
                 nc.sync.dma_start(out=out_dest(nb), in_=ost[:].rearrange("p h m l -> p h (m l)"))

@@ -69,8 +69,8 @@ def tile_gqa_pa_kernel(tc, x, cos, sin, Wq, Wkv, out_0, out_1, out_2):
 
         cos_sb = const.tile([P, M, 64], BF16, name="cos_sb")
         sin_sb = const.tile([P, M, 64], BF16, name="sin_sb")
-        nc.gpsimd.dma_start(out=cos_sb[:], in_=cosv)
-        nc.gpsimd.dma_start(out=sin_sb[:], in_=sinv)
+        nc.scalar.dma_start(out=cos_sb[:], in_=cosv)
+        nc.scalar.dma_start(out=sin_sb[:], in_=sinv)
         ident = const.tile([P, P], F32, name="ident")
         make_identity(nc, ident[:])
         identb = const.tile([P, P], BF16, name="identb")
@@ -114,18 +114,15 @@ def tile_gqa_pa_kernel(tc, x, cos, sin, Wq, Wkv, out_0, out_1, out_2):
             for g in range(G):
                 load_w(ORDER[i], g)
 
-        tcomp = const.tile([P, M, 2, 64, 2], F32, name="tcomp")
-        nc.gpsimd.tensor_scalar(out=tcomp[:, :, 0, :, 0], in0=cos_sb[:], scalar1=1.0, scalar2=0.0, op0=MULT, op1=ADD)
-        nc.gpsimd.tensor_scalar(out=tcomp[:, :, 0, :, 1], in0=sin_sb[:], scalar1=1.0, scalar2=0.0, op0=MULT, op1=ADD)
-        nc.gpsimd.tensor_scalar(out=tcomp[:, :, 1, :, 0], in0=sin_sb[:], scalar1=-1.0, scalar2=0.0, op0=MULT, op1=ADD)
-        nc.gpsimd.tensor_scalar(out=tcomp[:, :, 1, :, 1], in0=cos_sb[:], scalar1=1.0, scalar2=0.0, op0=MULT, op1=ADD)
-        tab = const.tile([P, M, 2, HB, HD], F32, name="tab")
-        for m in range(M):
-            nc.gpsimd.tensor_scalar(
-                out=tab[:, m],
-                in0=tcomp[:, m].rearrange("p q i y -> p q (i y)").unsqueeze(2).to_broadcast([P, 2, HB, HD]),
-                scalar1=1.0, scalar2=0.0, op0=MULT, op1=ADD,
-            )
+        tab = const.tile([P, M, 2, 2, HB, 64], BF16, name="tab")
+
+        def spread(t):
+            return t[:].unsqueeze(2).to_broadcast([P, M, HB, 64])
+
+        nc.vector.tensor_copy(out=tab[:, :, 0, 0], in_=spread(cos_sb))
+        nc.vector.tensor_copy(out=tab[:, :, 0, 1], in_=spread(sin_sb))
+        nc.vector.tensor_scalar(out=tab[:, :, 1, 0], in0=spread(sin_sb), scalar1=-1.0, scalar2=0.0, op0=MULT, op1=ADD)
+        nc.vector.tensor_copy(out=tab[:, :, 1, 1], in_=spread(cos_sb))
 
         xg = const.tile([P, M, G, P, 4], BF16, name="xg", align_bytes=64)
         xg32 = xg[:].bitcast(F32)
@@ -256,7 +253,7 @@ def tile_gqa_pa_kernel(tc, x, cos, sin, Wq, Wkv, out_0, out_1, out_2):
                 nc.vector.tensor_tensor(
                     out=z[:],
                     in0=a[:].rearrange("p (c q) -> p q c", q=2).unsqueeze(3).to_broadcast([P, 2, HB * 64, 2]),
-                    in1=tab[:, m].rearrange("p q h (i y) -> p q (h i) y", y=2),
+                    in1=tab[:, m].rearrange("p q y h i -> p q (h i) y"),
                     op=MULT,
                 )
                 if m not in add_v:

@@ -21,7 +21,7 @@ NW = 512
 HD = 128
 HB = 4
 
-PATHS = (("V", "V", "S", "V"), ("S", "S", "V", "S"), ("S", "S", "V", "S"), ("S", "S", "V", "S"), ("S", "S", "V", "S"), ("S", "S", "S", "S"))
+PATHS = (("V", "V", "S", "V"), ("S", "S", "V", "S"), ("S", "S", "S", "S"), ("S", "S", "V", "S"), ("S", "S", "S", "S"), ("S", "S", "S", "S"))
 ADD_V = ((2, 3), (2, 3), (2, 3), (2, 3), (2, 3), ())
 M_OUTER = (0, 1, 2, 3, 4)
 LEAD = 2

@@ -21,7 +21,7 @@ NW = 512
 HD = 128
 HB = 4
 
-PATHS = (("V", "V", "S", "V"), ("S", "S", "V", "S"), ("S", "S", "S", "S"), ("S", "S", "V", "S"), ("S", "S", "S", "S"), ("S", "S", "S", "S"))
+PATHS = (("V", "V", "S", "V"), ("V", "S", "V", "S"), ("S", "S", "V", "S"), ("S", "S", "S", "S"), ("S", "S", "S", "S"), ("S", "S", "S", "S"))
 ADD_V = ((2, 3), (2, 3), (2, 3), (2, 3), (2, 3), ())
 M_OUTER = (0, 1, 2, 3, 4)
 LEAD = 2
@@ -31,6 +31,7 @@ RAW2_BUFS = 6
 LOAD_LEAD = 4
 WG_BUFS = 4
 QW = 2
+NARROW_FROM = 5
 ACC_BUFS = 8
 AUX_BUFS = 0
 V_COPY = ("S", "S", "S", "S")
@@ -186,6 +187,15 @@ def tile_gqa_pa_kernel(tc, x, cos, sin, Wq, Wkv, out_0, out_1, out_2):
             ws = wcp.tile([P, G, NW], U8, name="ws", tag="ws", align_bytes=64)
             wq[nb] = (wc, ws)
             for h in range(G // QW):
+                if ORDER.index(nb) >= NARROW_FROM:
+                    for j in range(QW):
+                        g = h * QW + j
+                        nc.vector.quantize_mx(
+                            out=wc[:, g, :].bitcast(FP8X4),
+                            scales=ws[:, g, :],
+                            in_=wgs[(nb, h)][:, j].rearrange("p n t -> p (n t)"),
+                        )
+                    continue
                 nc.vector.quantize_mx(
                     out=wc[:, h * QW:(h + 1) * QW, :].rearrange("p g n -> p (g n)").bitcast(FP8X4),
                     scales=ws[:, h * QW:(h + 1) * QW, :].rearrange("p g n -> p (g n)"),

@@ -21,13 +21,13 @@ NW = 512
 HD = 128
 HB = 4
 
-PATHS = (("V", "V", "S", "V"), ("V", "S", "V", "S"), ("S", "S", "V", "S"), ("S", "S", "S", "S"), ("S", "S", "S", "S"), ("S", "S", "S", "S"))
+PATHS = (("V", "S", "V", "V"), ("V", "S", "V", "S"), ("S", "S", "V", "S"), ("S", "S", "S", "S"), ("S", "S", "S", "S"), ("S", "S", "S", "S"))
 ADD_V = ((2, 3), (2, 3), (2, 3), (2, 3), (2, 3), ())
 M_OUTER = (0, 1, 2, 3, 4)
 LEAD = 2
-RAW_BUFS = 8
-PAIR_FROM = 2
-RAW2_BUFS = 6
+RAW_BUFS = 20
+PAIR_FROM = 6
+RAW2_BUFS = 1
 LOAD_LEAD = 4
 WG_BUFS = 4
 QW = 2

@@ -14,283 +14,232 @@ MULT = mybir.AluOpType.mult
 ADD = mybir.AluOpType.add
 
 P = 128
-M = 4
-G = 4
-NB = 6
-NW = 512
-HD = 128
-HB = 4
+PACK = 4
+TILES = 4
+PASSES = 4
+BLOCKS = 6
+WIDTH = 512
+HEADS = 4
+LANES = 128
+PAIRS = 64
+KEY_BLOCK = 4
+VALUE_BLOCK = 5
 
-PATHS = (("V", "S", "V", "V"), ("V", "S", "V", "S"), ("S", "S", "V", "S"), ("S", "S", "S", "S"), ("S", "S", "S", "S"), ("S", "S", "S", "S"))
-ADD_V = ((2, 3), (2, 3), (2, 3), (2, 3), (2, 3), ())
-M_OUTER = (0, 1, 2, 3, 4)
-LEAD = 2
-RAW_BUFS = 20
-PAIR_FROM = 6
-RAW2_BUFS = 1
-LOAD_LEAD = 4
-WG_BUFS = 4
-QW = 2
-NARROW_FROM = 5
-ACC_BUFS = 8
-AUX_BUFS = 0
-V_COPY = ("S", "S", "S", "S")
-ORDER = (0, 1, 2, 3, 4, 5)
-PARTS_FROM = 4
+VECTOR_CHUNKS = ((0, 2, 3), (0, 2), (2,), (), (), ())
+
+GPSIMD_ADDS = (0, 1)
+
+REGROUP_AHEAD = 2
+LOAD_AHEAD = 4
+WIDE_QUANTISE = 2
+TILE_STORES_FROM = 4
 
 
 def tile_gqa_pa_kernel(tc, x, cos, sin, Wq, Wkv, out_0, out_1, out_2):
     nc = tc.nc
     with ExitStack() as ctx:
         const = ctx.enter_context(tc.tile_pool(name="const", bufs=1))
-        rawp = ctx.enter_context(tc.tile_pool(name="raw", bufs=RAW_BUFS))
-        raw2p = ctx.enter_context(tc.tile_pool(name="raw2", bufs=RAW2_BUFS))
-        wgp = ctx.enter_context(tc.tile_pool(name="wg", bufs=WG_BUFS))
-        wcp = ctx.enter_context(tc.tile_pool(name="wc", bufs=3))
-        zp = ctx.enter_context(tc.tile_pool(name="z", bufs=4))
-        op = ctx.enter_context(tc.tile_pool(name="o", bufs=3))
-        accp = ctx.enter_context(tc.psum_pool(name="accp", bufs=ACC_BUFS))
-        auxp = ctx.enter_context(tc.psum_pool(name="auxp", bufs=AUX_BUFS)) if AUX_BUFS else accp
-        aux_tag = "aux" if AUX_BUFS else "acc"
+        raw_pool = ctx.enter_context(tc.tile_pool(name="raw", bufs=TILES + 3 * PASSES))
+        raw_kv_pool = ctx.enter_context(tc.tile_pool(name="raw_kv", bufs=PASSES))
+        grouped_pool = ctx.enter_context(tc.tile_pool(name="grouped", bufs=REGROUP_AHEAD * PASSES // WIDE_QUANTISE))
+        code_pool = ctx.enter_context(tc.tile_pool(name="codes", bufs=3))
+        product_pool = ctx.enter_context(tc.tile_pool(name="products", bufs=4))
+        result_pool = ctx.enter_context(tc.tile_pool(name="results", bufs=3))
+        psum = ctx.enter_context(tc.psum_pool(name="psum", bufs=8))
 
-        xv = x.rearrange("b (p m) k -> p (b m) k", m=M)
-        cosv = cos.rearrange("(p m) i -> p m i", m=M)
-        sinv = sin.rearrange("(p m) i -> p m i", m=M)
-        outv = [o.rearrange("b h (p m) l -> p (b h) (m l)", m=M) for o in (out_0, out_1, out_2)]
+        x_view = x.rearrange("b (p m) k -> p (b m) k", m=TILES)
+        out_views = [o.rearrange("b h (p m) l -> p (b h) (m l)", m=TILES) for o in (out_0, out_1, out_2)]
 
-        def w_source(nb):
-            if nb < 4:
-                return Wq, nb * NW
-            return Wkv, (nb - 4) * NW
+        def out_view(block):
+            if block < 4:
+                return out_views[0][:, block * HEADS:(block + 1) * HEADS, :]
+            return out_views[block - 3][:, :, :]
 
-        def out_dest(nb):
-            if nb < 4:
-                return outv[0][:, nb * HB:(nb + 1) * HB, :]
-            return outv[nb - 3][:, :, :]
+        cos_sb = const.tile([P, TILES, PAIRS], BF16, name="cos_sb")
+        sin_sb = const.tile([P, TILES, PAIRS], BF16, name="sin_sb")
+        nc.scalar.dma_start(out=cos_sb[:], in_=cos.rearrange("(p m) i -> p m i", m=TILES))
+        nc.scalar.dma_start(out=sin_sb[:], in_=sin.rearrange("(p m) i -> p m i", m=TILES))
+        identity = const.tile([P, P], F32, name="identity")
+        make_identity(nc, identity[:])
 
-        cos_sb = const.tile([P, M, 64], BF16, name="cos_sb")
-        sin_sb = const.tile([P, M, 64], BF16, name="sin_sb")
-        nc.scalar.dma_start(out=cos_sb[:], in_=cosv)
-        nc.scalar.dma_start(out=sin_sb[:], in_=sinv)
-        ident = const.tile([P, P], F32, name="ident")
-        make_identity(nc, ident[:])
-        identb = const.tile([P, P], BF16, name="identb")
-        make_identity(nc, identb[:])
-
-        x_sb = {}
-        raw = {}
+        x_raw = {}
+        w_raw = {}
 
         def load_x(m):
-            x_sb[m] = rawp.tile([P, 2048], BF16, name="xs", tag="rw")
-            nc.sync.dma_start(out=x_sb[m][:], in_=xv[:, m, :])
+            x_raw[m] = raw_pool.tile([P, PASSES * WIDTH], BF16, name="x_raw", tag="raw")
+            nc.sync.dma_start(out=x_raw[m][:], in_=x_view[:, m, :])
 
-        def load_w(nb, g):
-            src, c0 = w_source(nb)
-            place = ORDER.index(nb)
-            if place >= PAIR_FROM:
-                if (place - PAIR_FROM) % 2 == 1:
-                    return
-                assert ORDER[place + 1] == nb + 1
-                rw2 = raw2p.tile([P, 4, 2 * NW], BF16, name="rw2", tag="rw2")
-                nc.sync.dma_start(
-                    out=rw2[:],
-                    in_=src[g * 512:(g + 1) * 512, c0:c0 + 2 * NW].rearrange("(p j) n -> p j n", j=4),
-                )
-                raw[(nb, g)] = rw2[:, :, 0:NW]
-                raw[(nb + 1, g)] = rw2[:, :, NW:2 * NW]
+        def load_block(block):
+            if block == VALUE_BLOCK:
                 return
-            rw = rawp.tile([P, 4, NW], BF16, name="rw", tag="rw")
-            nc.sync.dma_start(
-                out=rw[:],
-                in_=src[g * 512:(g + 1) * 512, c0:c0 + NW].rearrange("(p j) n -> p j n", j=4),
-            )
-            raw[(nb, g)] = rw[:]
+            for g in range(PASSES):
+                if block == KEY_BLOCK:
+                    both = raw_kv_pool.tile([P, PACK, 2 * WIDTH], BF16, name="kv_raw", tag="raw_kv")
+                    nc.sync.dma_start(out=both[:], in_=Wkv[g * 512:(g + 1) * 512, :].rearrange("(p t) n -> p t n", t=PACK))
+                    w_raw[(KEY_BLOCK, g)] = both[:, :, 0:WIDTH]
+                    w_raw[(VALUE_BLOCK, g)] = both[:, :, WIDTH:2 * WIDTH]
+                    continue
+                chunk = raw_pool.tile([P, PACK, WIDTH], BF16, name="w_raw", tag="raw")
+                nc.sync.dma_start(
+                    out=chunk[:],
+                    in_=Wq[g * 512:(g + 1) * 512, block * WIDTH:(block + 1) * WIDTH].rearrange("(p t) n -> p t n", t=PACK),
+                )
+                w_raw[(block, g)] = chunk[:]
 
         load_x(0)
-        for g in range(G):
-            load_w(ORDER[0], g)
-        for m in range(1, M):
+        load_block(0)
+        for m in range(1, TILES):
             load_x(m)
-        for i in range(1, LOAD_LEAD):
-            for g in range(G):
-                load_w(ORDER[i], g)
+        for block in range(1, LOAD_AHEAD):
+            load_block(block)
 
-        tab = const.tile([P, M, 2, 2, HB, 64], BF16, name="tab")
+        table = const.tile([P, TILES, 2, 2, HEADS, PAIRS], BF16, name="table")
 
-        def spread(t):
-            return t[:].unsqueeze(2).to_broadcast([P, M, HB, 64])
+        def for_each_head(values):
+            return values[:].unsqueeze(2).to_broadcast([P, TILES, HEADS, PAIRS])
 
-        nc.vector.tensor_copy(out=tab[:, :, 0, 0], in_=spread(cos_sb))
-        nc.vector.tensor_copy(out=tab[:, :, 0, 1], in_=spread(sin_sb))
-        nc.vector.tensor_scalar(out=tab[:, :, 1, 0], in0=spread(sin_sb), scalar1=-1.0, scalar2=0.0, op0=MULT, op1=ADD)
-        nc.vector.tensor_copy(out=tab[:, :, 1, 1], in_=spread(cos_sb))
+        nc.vector.tensor_copy(out=table[:, :, 0, 0], in_=for_each_head(cos_sb))
+        nc.vector.tensor_copy(out=table[:, :, 0, 1], in_=for_each_head(sin_sb))
+        nc.vector.tensor_scalar(out=table[:, :, 1, 0], in0=for_each_head(sin_sb),
+                                scalar1=-1.0, scalar2=0.0, op0=MULT, op1=ADD)
+        nc.vector.tensor_copy(out=table[:, :, 1, 1], in_=for_each_head(cos_sb))
 
-        xg = const.tile([P, M, G, P, 4], BF16, name="xg", align_bytes=64)
-        xg32 = xg[:].bitcast(F32)
-        x_codes = const.tile([P, M, G, P], U32, name="x_codes", align_bytes=64)
-        x_scales = const.tile([P, M, G, P], U8, name="x_scales", align_bytes=64)
+        x_grouped = const.tile([P, TILES, PASSES, P, PACK], BF16, name="x_grouped", align_bytes=64)
+        x_grouped_words = x_grouped[:].bitcast(F32)
+        x_codes = const.tile([P, TILES, PASSES, P], U32, name="x_codes", align_bytes=64)
+        x_scales = const.tile([P, TILES, PASSES, P], U8, name="x_scales", align_bytes=64)
 
-        def prep_x(m):
-            words = x_sb[m][:].bitcast(F32).rearrange("p (g q u) -> p g u q", g=G, u=2)
-            for gh in range(2):
-                bank = auxp.tile([P, 2, 2, P], F32, name="xt", tag=aux_tag)
-                for gl in range(2):
+        def prepare_x(m):
+            words = x_raw[m][:].bitcast(F32).rearrange("s (g p u) -> s g u p", g=PASSES, u=2)
+            for half in range(2):
+                bank = psum.tile([P, 2, 2, P], F32, name="x_bank", tag="bank")
+                for g in range(2):
                     for u in range(2):
-                        nc.tensor.transpose(bank[:, gl, u, :], words[:, 2 * gh + gl, u, :], ident[:])
-                dst = xg32[:, m, 2 * gh:2 * gh + 2, :, :]
-                srcv = bank[:].rearrange("p g u s -> p g s u")
-                nc.scalar.copy(out=dst, in_=srcv)
+                        nc.tensor.transpose(bank[:, g, u, :], words[:, 2 * half + g, u, :], identity[:])
+                nc.scalar.copy(out=x_grouped_words[:, m, 2 * half:2 * half + 2, :, :],
+                               in_=bank[:].rearrange("p g u s -> p g s u"))
             nc.vector.quantize_mx(
                 out=x_codes[:, m].rearrange("p g s -> p (g s)").bitcast(FP8X4),
                 scales=x_scales[:, m].rearrange("p g s -> p (g s)"),
-                in_=xg[:, m].rearrange("p g s t -> p (g s t)"),
+                in_=x_grouped[:, m].rearrange("p g s t -> p (g s t)"),
             )
 
-        wq = {}
-        wgs = {}
-        pending = []
+        w_grouped = {}
+        w_codes = {}
 
-        def regroup(nb):
-            for g in range(G):
-                path = PATHS[ORDER.index(nb)][g]
-                if g % QW == 0:
-                    wgt = wgp.tile([P, QW, NW, 4], BF16, name="wgt", tag="wg", align_bytes=64)
-                    wgs[(nb, g // QW)] = wgt
-                wg = wgs[(nb, g // QW)][:, g % QW]
-                dst = wg.rearrange("p (c i) t -> p c t i", i=4)
-                srcv = raw[(nb, g)].rearrange("p t (c i) -> p c t i", i=4)
-                if path == "V":
-                    nc.vector.tensor_copy(out=dst, in_=srcv)
-                elif path == "S":
-                    nc.scalar.copy(out=dst, in_=srcv)
+        def regroup(block):
+            for g in range(PASSES):
+                if g % WIDE_QUANTISE == 0:
+                    w_grouped[(block, g // WIDE_QUANTISE)] = grouped_pool.tile(
+                        [P, WIDE_QUANTISE, WIDTH, PACK], BF16, name="w_grouped", tag="grouped", align_bytes=64)
+                target = w_grouped[(block, g // WIDE_QUANTISE)][:, g % WIDE_QUANTISE]
+                target = target.rearrange("p (c i) t -> p c t i", i=4)
+                source = w_raw[(block, g)].rearrange("p t (c i) -> p c t i", i=4)
+                if g in VECTOR_CHUNKS[block]:
+                    nc.vector.tensor_copy(out=target, in_=source)
                 else:
-                    flat = wg.rearrange("p n t -> p (n t)")
-                    for half in range(2):
-                        wi = auxp.tile([P, 2, P, 4], BF16, name="wi", tag=aux_tag)
-                        for q in range(2):
-                            c0 = (2 * half + q) * P
-                            nc.tensor.matmul(
-                                out=wi[:, q],
-                                lhsT=identb[:],
-                                rhs=raw[(nb, g)][:, :, c0:c0 + P].rearrange("p t c -> p c t"),
-                                start=True, stop=True,
-                            )
-                        o_ = flat[:, half * 1024:(half + 1) * 1024]
-                        i_ = wi[:].rearrange("p q c t -> p (q c t)")
-                        if path == "PS":
-                            nc.scalar.copy(out=o_, in_=i_)
-                        else:
-                            pending.append((o_, i_))
+                    nc.scalar.copy(out=target, in_=source)
 
-        def quant(nb):
-            wc = wcp.tile([P, G, NW], U32, name="wc", tag="wc", align_bytes=64)
-            ws = wcp.tile([P, G, NW], U8, name="ws", tag="ws", align_bytes=64)
-            wq[nb] = (wc, ws)
-            for h in range(G // QW):
-                if ORDER.index(nb) >= NARROW_FROM:
-                    for j in range(QW):
-                        g = h * QW + j
+        def quantise(block):
+            codes = code_pool.tile([P, PASSES, WIDTH], U32, name="codes", tag="codes", align_bytes=64)
+            scales = code_pool.tile([P, PASSES, WIDTH], U8, name="scales", tag="scales", align_bytes=64)
+            w_codes[block] = (codes, scales)
+            for pair in range(PASSES // WIDE_QUANTISE):
+                first = pair * WIDE_QUANTISE
+                if block == BLOCKS - 1:
+                    for j in range(WIDE_QUANTISE):
                         nc.vector.quantize_mx(
-                            out=wc[:, g, :].bitcast(FP8X4),
-                            scales=ws[:, g, :],
-                            in_=wgs[(nb, h)][:, j].rearrange("p n t -> p (n t)"),
+                            out=codes[:, first + j, :].bitcast(FP8X4),
+                            scales=scales[:, first + j, :],
+                            in_=w_grouped[(block, pair)][:, j].rearrange("p n t -> p (n t)"),
                         )
                     continue
                 nc.vector.quantize_mx(
-                    out=wc[:, h * QW:(h + 1) * QW, :].rearrange("p g n -> p (g n)").bitcast(FP8X4),
-                    scales=ws[:, h * QW:(h + 1) * QW, :].rearrange("p g n -> p (g n)"),
-                    in_=wgs[(nb, h)][:].rearrange("p g n t -> p (g n t)"),
+                    out=codes[:, first:first + WIDE_QUANTISE, :].rearrange("p g n -> p (g n)").bitcast(FP8X4),
+                    scales=scales[:, first:first + WIDE_QUANTISE, :].rearrange("p g n -> p (g n)"),
+                    in_=w_grouped[(block, pair)][:].rearrange("p g n t -> p (g n t)"),
                 )
 
-        acc = {}
+        sums = {}
 
-        def mx_pass(nb, m, g):
-            wc, ws = wq[nb]
+        def one_pass(block, m, g):
+            codes, scales = w_codes[block]
             nc.tensor.matmul_mx(
-                out=acc[(nb, m)][:],
+                out=sums[(block, m)][:],
                 lhsT=x_codes[:, m, g, :].bitcast(FP8X4),
                 lhsT_scale=x_scales[:, m, g, :],
-                rhs=wc[:, g, :].bitcast(FP8X4),
-                rhs_scale=ws[:, g, :],
+                rhs=codes[:, g, :].bitcast(FP8X4),
+                rhs_scale=scales[:, g, :],
                 start=(g == 0),
-                stop=(g == G - 1),
+                stop=(g == PASSES - 1),
             )
 
-        def mx(nb, m_outer):
-            if m_outer:
-                for m in range(M):
-                    acc[(nb, m)] = accp.tile([P, NW], F32, name="acc", tag="acc")
-                    for g in range(G):
-                        mx_pass(nb, m, g)
+        def multiply(block):
+            if block < BLOCKS - 1:
+                for m in range(TILES):
+                    sums[(block, m)] = psum.tile([P, WIDTH], F32, name="sums", tag="bank")
+                    for g in range(PASSES):
+                        one_pass(block, m, g)
             else:
-                for m in range(M):
-                    acc[(nb, m)] = accp.tile([P, NW], F32, name="acc", tag="acc")
-                for g in range(G):
-                    for m in range(M):
-                        mx_pass(nb, m, g)
+                for m in range(TILES):
+                    sums[(block, m)] = psum.tile([P, WIDTH], F32, name="sums", tag="bank")
+                for g in range(PASSES):
+                    for m in range(TILES):
+                        one_pass(block, m, g)
 
-        def finish(nb):
-            ost = op.tile([P, HB, M, HD], F32, name="ost", tag="ost")
-            parts = ORDER.index(nb) >= PARTS_FROM
-            add_v = ADD_V[ORDER.index(nb)]
+        def finish(block):
+            result = result_pool.tile([P, HEADS, TILES, LANES], F32, name="result", tag="result")
+            tile_by_tile = block >= TILE_STORES_FROM
 
-            def done(m):
-                if parts:
-                    nc.sync.dma_start(out=out_dest(nb)[:, :, m * HD:(m + 1) * HD], in_=ost[:, :, m, :])
+            def tile_done(m):
+                if tile_by_tile:
+                    nc.sync.dma_start(out=out_view(block)[:, :, m * LANES:(m + 1) * LANES], in_=result[:, :, m, :])
 
-            def add(eng, m, z):
-                eng.tensor_tensor(
-                    out=ost[:, :, m, :],
-                    in0=z[:, 0].rearrange("p (h i) y -> p h (i y)", h=HB),
-                    in1=z[:, 1].rearrange("p (h i) y -> p h (i y)", h=HB),
+            def add(engine, m, products):
+                engine.tensor_tensor(
+                    out=result[:, :, m, :],
+                    in0=products[:, 0].rearrange("p (h i) y -> p h (i y)", h=HEADS),
+                    in1=products[:, 1].rearrange("p (h i) y -> p h (i y)", h=HEADS),
                     op=ADD,
                 )
-                done(m)
+                tile_done(m)
 
-            zs = {}
-            for m in range(M):
-                a = acc[(nb, m)]
-                if nb == NB - 1:
-                    av = a[:].rearrange("p (h l) -> p h l", h=HB)
-                    if V_COPY[m] == "S":
-                        nc.scalar.copy(out=ost[:, :, m, :], in_=av)
-                    else:
-                        nc.vector.tensor_copy(out=ost[:, :, m, :], in_=av)
-                    done(m)
+            waiting = {}
+            for m in range(TILES):
+                bank = sums[(block, m)]
+                if block == VALUE_BLOCK:
+                    nc.scalar.copy(out=result[:, :, m, :], in_=bank[:].rearrange("p (h l) -> p h l", h=HEADS))
+                    tile_done(m)
                     continue
-                z = zp.tile([P, 2, HB * 64, 2], F32, name="z", tag="z")
-                zs[m] = z
+                products = product_pool.tile([P, 2, HEADS * PAIRS, 2], F32, name="products", tag="products")
                 nc.vector.tensor_tensor(
-                    out=z[:],
-                    in0=a[:].rearrange("p (c q) -> p q c", q=2).unsqueeze(3).to_broadcast([P, 2, HB * 64, 2]),
-                    in1=tab[:, m].rearrange("p q y h i -> p q (h i) y"),
+                    out=products[:],
+                    in0=bank[:].rearrange("p (c q) -> p q c", q=2).unsqueeze(3).to_broadcast([P, 2, HEADS * PAIRS, 2]),
+                    in1=table[:, m].rearrange("p q y h i -> p q (h i) y"),
                     op=MULT,
                 )
-                if m not in add_v:
-                    add(nc.gpsimd, m, z)
-            for o_, i_ in pending:
-                nc.vector.tensor_copy(out=o_, in_=i_)
-            pending.clear()
-            for m in sorted(zs):
-                if m in add_v:
-                    add(nc.vector, m, zs[m])
-            if not parts:
-                nc.sync.dma_start(out=out_dest(nb), in_=ost[:].rearrange("p h m l -> p h (m l)"))
+                if m in GPSIMD_ADDS:
+                    add(nc.gpsimd, m, products)
+                else:
+                    waiting[m] = products
+            for m in sorted(waiting):
+                add(nc.vector, m, waiting[m])
+            if not tile_by_tile:
+                nc.sync.dma_start(out=out_view(block), in_=result[:].rearrange("p h m l -> p h (m l)"))
 
-        prep_x(0)
-        regroup(ORDER[0])
-        quant(ORDER[0])
-        for m in range(1, M):
-            prep_x(m)
-        for i in range(1, LEAD):
-            regroup(ORDER[i])
-        for i in range(NB):
-            if i + LEAD < NB:
-                regroup(ORDER[i + LEAD])
-            if i + 1 < NB:
-                quant(ORDER[i + 1])
-            mx(ORDER[i], m_outer=(i in M_OUTER))
-            if i + LOAD_LEAD < NB:
-                for g in range(G):
-                    load_w(ORDER[i + LOAD_LEAD], g)
-            finish(ORDER[i])
+        prepare_x(0)
+        regroup(0)
+        quantise(0)
+        for m in range(1, TILES):
+            prepare_x(m)
+        for block in range(1, REGROUP_AHEAD):
+            regroup(block)
+        for block in range(BLOCKS):
+            if block + REGROUP_AHEAD < BLOCKS:
+                regroup(block + REGROUP_AHEAD)
+            if block + 1 < BLOCKS:
+                quantise(block + 1)
+            multiply(block)
+            if block + LOAD_AHEAD < BLOCKS:
+                load_block(block + LOAD_AHEAD)
+            finish(block)

@@ -22,17 +22,15 @@ WIDTH = 512
 HEADS = 4
 LANES = 128
 PAIRS = 64
-KEY_BLOCK = 4
-VALUE_BLOCK = 5
+VALUE_BLOCK = 4
+KEY_BLOCK = 5
 
-VECTOR_CHUNKS = ((0, 2, 3), (0, 2), (2,), (), (), ())
+VECTOR_CHUNKS = ((0, 2, 3), (0, 2), (2,), (2,), (), ())
 
 GPSIMD_ADDS = (0, 1)
 
 REGROUP_AHEAD = 2
-LOAD_AHEAD = 4
 WIDE_QUANTISE = 2
-TILE_STORES_FROM = 4
 
 
 def tile_gqa_pa_kernel(tc, x, cos, sin, Wq, Wkv, out_0, out_1, out_2):
@@ -53,7 +51,7 @@ def tile_gqa_pa_kernel(tc, x, cos, sin, Wq, Wkv, out_0, out_1, out_2):
         def out_view(block):
             if block < 4:
                 return out_views[0][:, block * HEADS:(block + 1) * HEADS, :]
-            return out_views[block - 3][:, :, :]
+            return out_views[1 if block == KEY_BLOCK else 2][:, :, :]
 
         cos_sb = const.tile([P, TILES, PAIRS], BF16, name="cos_sb")
         sin_sb = const.tile([P, TILES, PAIRS], BF16, name="sin_sb")
@@ -61,6 +59,7 @@ def tile_gqa_pa_kernel(tc, x, cos, sin, Wq, Wkv, out_0, out_1, out_2):
         nc.scalar.dma_start(out=sin_sb[:], in_=sin.rearrange("(p m) i -> p m i", m=TILES))
         identity = const.tile([P, P], F32, name="identity")
         make_identity(nc, identity[:])
+        ctx.enter_context(tc.manual_schedule())
 
         x_raw = {}
         w_raw = {}
@@ -70,10 +69,10 @@ def tile_gqa_pa_kernel(tc, x, cos, sin, Wq, Wkv, out_0, out_1, out_2):
             nc.sync.dma_start(out=x_raw[m][:], in_=x_view[:, m, :])
 
         def load_block(block):
-            if block == VALUE_BLOCK:
+            if block == KEY_BLOCK:
                 return
             for g in range(PASSES):
-                if block == KEY_BLOCK:
+                if block == VALUE_BLOCK:
                     both = raw_kv_pool.tile([P, PACK, 2 * WIDTH], BF16, name="kv_raw", tag="raw_kv")
                     nc.sync.dma_start(out=both[:], in_=Wkv[g * 512:(g + 1) * 512, :].rearrange("(p t) n -> p t n", t=PACK))
                     w_raw[(KEY_BLOCK, g)] = both[:, :, 0:WIDTH]
@@ -90,7 +89,7 @@ def tile_gqa_pa_kernel(tc, x, cos, sin, Wq, Wkv, out_0, out_1, out_2):
         load_block(0)
         for m in range(1, TILES):
             load_x(m)
-        for block in range(1, LOAD_AHEAD):
+        for block in range(1, BLOCKS):
             load_block(block)
 
         table = const.tile([P, TILES, 2, 2, HEADS, PAIRS], BF16, name="table")
@@ -175,71 +174,91 @@ def tile_gqa_pa_kernel(tc, x, cos, sin, Wq, Wkv, out_0, out_1, out_2):
             )
 
         def multiply(block):
-            if block < BLOCKS - 1:
-                for m in range(TILES):
-                    sums[(block, m)] = psum.tile([P, WIDTH], F32, name="sums", tag="bank")
-                    for g in range(PASSES):
-                        one_pass(block, m, g)
-            else:
-                for m in range(TILES):
-                    sums[(block, m)] = psum.tile([P, WIDTH], F32, name="sums", tag="bank")
-                for g in range(PASSES):
-                    for m in range(TILES):
-                        one_pass(block, m, g)
-
-        def finish(block):
-            result = result_pool.tile([P, HEADS, TILES, LANES], F32, name="result", tag="result")
-            tile_by_tile = block >= TILE_STORES_FROM
-
-            def tile_done(m):
-                if tile_by_tile:
-                    nc.sync.dma_start(out=out_view(block)[:, :, m * LANES:(m + 1) * LANES], in_=result[:, :, m, :])
-
-            def add(engine, m, products):
-                engine.tensor_tensor(
-                    out=result[:, :, m, :],
-                    in0=products[:, 0].rearrange("p (h i) y -> p h (i y)", h=HEADS),
-                    in1=products[:, 1].rearrange("p (h i) y -> p h (i y)", h=HEADS),
-                    op=ADD,
-                )
-                tile_done(m)
-
-            waiting = {}
             for m in range(TILES):
-                bank = sums[(block, m)]
-                if block == VALUE_BLOCK:
-                    nc.scalar.copy(out=result[:, :, m, :], in_=bank[:].rearrange("p (h l) -> p h l", h=HEADS))
-                    tile_done(m)
-                    continue
-                products = product_pool.tile([P, 2, HEADS * PAIRS, 2], F32, name="products", tag="products")
-                nc.vector.tensor_tensor(
-                    out=products[:],
-                    in0=bank[:].rearrange("p (c q) -> p q c", q=2).unsqueeze(3).to_broadcast([P, 2, HEADS * PAIRS, 2]),
-                    in1=table[:, m].rearrange("p q y h i -> p q (h i) y"),
-                    op=MULT,
-                )
-                if m in GPSIMD_ADDS:
-                    add(nc.gpsimd, m, products)
-                else:
-                    waiting[m] = products
-            for m in sorted(waiting):
-                add(nc.vector, m, waiting[m])
-            if not tile_by_tile:
-                nc.sync.dma_start(out=out_view(block), in_=result[:].rearrange("p h m l -> p h (m l)"))
+                sums[(block, m)] = psum.tile([P, WIDTH], F32, name="sums", tag="bank")
+                for g in range(PASSES):
+                    one_pass(block, m, g)
+
+        results = {}
+        products_of = {}
+
+        def rotate_multiply(block, m):
+            if block not in results:
+                results[block] = result_pool.tile([P, HEADS, TILES, LANES], F32, name="result", tag="result")
+            products = product_pool.tile([P, 2, HEADS * PAIRS, 2], F32, name="products", tag="products")
+            products_of[(block, m)] = products
+            nc.vector.tensor_tensor(
+                out=products[:],
+                in0=sums[(block, m)][:].rearrange("p (c q) -> p q c", q=2).unsqueeze(3).to_broadcast([P, 2, HEADS * PAIRS, 2]),
+                in1=table[:, m].rearrange("p q y h i -> p q (h i) y"),
+                op=MULT,
+            )
+
+        def rotate_add(block, m):
+            engine = nc.gpsimd if m in GPSIMD_ADDS else nc.vector
+            products = products_of[(block, m)]
+            engine.tensor_tensor(
+                out=results[block][:, :, m, :],
+                in0=products[:, 0].rearrange("p (h i) y -> p h (i y)", h=HEADS),
+                in1=products[:, 1].rearrange("p (h i) y -> p h (i y)", h=HEADS),
+                op=ADD,
+            )
+
+        def store(block):
+            nc.sync.dma_start(out=out_view(block), in_=results[block][:].rearrange("p h m l -> p h (m l)"))
+
+        def store_tile(block, m):
+            nc.sync.dma_start(out=out_view(block)[:, :, m * LANES:(m + 1) * LANES], in_=results[block][:, :, m, :])
+
+        def copy_values():
+            results[VALUE_BLOCK] = result_pool.tile([P, HEADS, TILES, LANES], F32, name="result", tag="result")
+            for m in range(TILES):
+                nc.scalar.copy(out=results[VALUE_BLOCK][:, :, m, :],
+                               in_=sums[(VALUE_BLOCK, m)][:].rearrange("p (h l) -> p h l", h=HEADS))
 
         prepare_x(0)
         regroup(0)
         quantise(0)
         for m in range(1, TILES):
             prepare_x(m)
-        for block in range(1, REGROUP_AHEAD):
-            regroup(block)
-        for block in range(BLOCKS):
-            if block + REGROUP_AHEAD < BLOCKS:
-                regroup(block + REGROUP_AHEAD)
-            if block + 1 < BLOCKS:
-                quantise(block + 1)
+        multiply(0)
+        rotate_multiply(0, 0)
+        rotate_add(0, 0)
+        rotate_multiply(0, 1)
+        rotate_add(0, 1)
+        regroup(1)
+        rotate_multiply(0, 2)
+        rotate_multiply(0, 3)
+        rotate_add(0, 2)
+        rotate_add(0, 3)
+        store(0)
+        quantise(1)
+        for block in range(1, VALUE_BLOCK):
+            regroup(block + 1)
+            quantise(block + 1)
             multiply(block)
-            if block + LOAD_AHEAD < BLOCKS:
-                load_block(block + LOAD_AHEAD)
-            finish(block)
+            for m in range(TILES):
+                rotate_multiply(block, m)
+                if m in GPSIMD_ADDS:
+                    rotate_add(block, m)
+            rotate_add(block, 2)
+            if block < VALUE_BLOCK - 1:
+                rotate_add(block, 3)
+                store(block)
+        regroup(KEY_BLOCK)
+        quantise(KEY_BLOCK)
+        rotate_add(VALUE_BLOCK - 1, 3)
+        store(VALUE_BLOCK - 1)
+        multiply(VALUE_BLOCK)
+        copy_values()
+        store(VALUE_BLOCK)
+        multiply(KEY_BLOCK)
+        for m in range(TILES):
+            rotate_multiply(KEY_BLOCK, m)
+            if m in GPSIMD_ADDS:
+                rotate_add(KEY_BLOCK, m)
+                store_tile(KEY_BLOCK, m)
+        for m in range(TILES):
+            if m not in GPSIMD_ADDS:
+                rotate_add(KEY_BLOCK, m)
+                store_tile(KEY_BLOCK, m)

@@ -92,16 +92,12 @@ def tile_gqa_pa_kernel(tc, x, cos, sin, Wq, Wkv, out_0, out_1, out_2):
         for block in range(1, BLOCKS):
             load_block(block)
 
-        table = const.tile([P, TILES, 2, 2, HEADS, PAIRS], BF16, name="table")
-
-        def for_each_head(values):
-            return values[:].unsqueeze(2).to_broadcast([P, TILES, HEADS, PAIRS])
-
-        nc.vector.tensor_copy(out=table[:, :, 0, 0], in_=for_each_head(cos_sb))
-        nc.vector.tensor_copy(out=table[:, :, 0, 1], in_=for_each_head(sin_sb))
-        nc.vector.tensor_scalar(out=table[:, :, 1, 0], in0=for_each_head(sin_sb),
+        table = const.tile([P, TILES, 2, PAIRS, 2], BF16, name="table")
+        nc.vector.tensor_copy(out=table[:, :, 0, :, 0], in_=cos_sb[:])
+        nc.vector.tensor_copy(out=table[:, :, 0, :, 1], in_=sin_sb[:])
+        nc.vector.tensor_scalar(out=table[:, :, 1, :, 0], in0=sin_sb[:],
                                 scalar1=-1.0, scalar2=0.0, op0=MULT, op1=ADD)
-        nc.vector.tensor_copy(out=table[:, :, 1, 1], in_=for_each_head(cos_sb))
+        nc.vector.tensor_copy(out=table[:, :, 1, :, 1], in_=cos_sb[:])
 
         x_grouped = const.tile([P, TILES, PASSES, P, PACK], BF16, name="x_grouped", align_bytes=64)
         x_grouped_words = x_grouped[:].bitcast(F32)
@@ -185,12 +181,12 @@ def tile_gqa_pa_kernel(tc, x, cos, sin, Wq, Wkv, out_0, out_1, out_2):
         def rotate_multiply(block, m):
             if block not in results:
                 results[block] = result_pool.tile([P, HEADS, TILES, LANES], F32, name="result", tag="result")
-            products = product_pool.tile([P, 2, HEADS * PAIRS, 2], F32, name="products", tag="products")
+            products = product_pool.tile([P, 2, HEADS, PAIRS, 2], F32, name="products", tag="products")
             products_of[(block, m)] = products
             nc.vector.tensor_tensor(
                 out=products[:],
-                in0=sums[(block, m)][:].rearrange("p (c q) -> p q c", q=2).unsqueeze(3).to_broadcast([P, 2, HEADS * PAIRS, 2]),
-                in1=table[:, m].rearrange("p q y h i -> p q (h i) y"),
+                in0=sums[(block, m)][:].rearrange("p (h i q) -> p q h i", h=HEADS, q=2).unsqueeze(4).to_broadcast([P, 2, HEADS, PAIRS, 2]),
+                in1=table[:, m].unsqueeze(2).to_broadcast([P, 2, HEADS, PAIRS, 2]),
                 op=MULT,
             )
 
@@ -199,8 +195,8 @@ def tile_gqa_pa_kernel(tc, x, cos, sin, Wq, Wkv, out_0, out_1, out_2):
             products = products_of[(block, m)]
             engine.tensor_tensor(
                 out=results[block][:, :, m, :],
-                in0=products[:, 0].rearrange("p (h i) y -> p h (i y)", h=HEADS),
-                in1=products[:, 1].rearrange("p (h i) y -> p h (i y)", h=HEADS),
+                in0=products[:, 0].rearrange("p h i y -> p h (i y)"),
+                in1=products[:, 1].rearrange("p h i y -> p h (i y)"),
                 op=ADD,
             )
 

@@ -25,7 +25,7 @@ PAIRS = 64
 VALUE_BLOCK = 4
 KEY_BLOCK = 5
 
-VECTOR_CHUNKS = ((0, 2, 3), (0, 2), (2,), (2,), (), ())
+VECTOR_CHUNKS = ((0, 2, 3), (0, 2), (2,), (), (), ())
 
 GPSIMD_ADDS = (0, 1)
 

@@ -25,7 +25,8 @@ PAIRS = 64
 VALUE_BLOCK = 4
 KEY_BLOCK = 5
 
-VECTOR_CHUNKS = ((0, 2, 3), (0, 2), (2,), (), (), ())
+VECTOR_CHUNKS = ((0, 2, 3), (0, 2), (), (), (), ())
+TENSOR_CHUNKS = ((), (), (3,), (3,), (3,), (3,))
 
 GPSIMD_ADDS = (0, 1)
 
@@ -43,7 +44,8 @@ def tile_gqa_pa_kernel(tc, x, cos, sin, Wq, Wkv, out_0, out_1, out_2):
         code_pool = ctx.enter_context(tc.tile_pool(name="codes", bufs=3))
         product_pool = ctx.enter_context(tc.tile_pool(name="products", bufs=4))
         result_pool = ctx.enter_context(tc.tile_pool(name="results", bufs=3))
-        psum = ctx.enter_context(tc.psum_pool(name="psum", bufs=8))
+        psum = ctx.enter_context(tc.psum_pool(name="psum", bufs=6))
+        regroup_psum = ctx.enter_context(tc.psum_pool(name="regroup_psum", bufs=2))
 
         x_view = x.rearrange("b (p m) k -> p (b m) k", m=TILES)
         out_views = [o.rearrange("b h (p m) l -> p (b h) (m l)", m=TILES) for o in (out_0, out_1, out_2)]
@@ -59,6 +61,8 @@ def tile_gqa_pa_kernel(tc, x, cos, sin, Wq, Wkv, out_0, out_1, out_2):
         nc.scalar.dma_start(out=sin_sb[:], in_=sin.rearrange("(p m) i -> p m i", m=TILES))
         identity = const.tile([P, P], F32, name="identity")
         make_identity(nc, identity[:])
+        identity_bf16 = const.tile([P, P], BF16, name="identity_bf16")
+        make_identity(nc, identity_bf16[:])
         ctx.enter_context(tc.manual_schedule())
 
         x_raw = {}
@@ -122,12 +126,34 @@ def tile_gqa_pa_kernel(tc, x, cos, sin, Wq, Wkv, out_0, out_1, out_2):
         w_grouped = {}
         w_codes = {}
 
+        regroup_banks = {}
+
+        def regroup_on_tensor(block):
+            for g in TENSOR_CHUNKS[block]:
+                for half in range(2):
+                    bank = regroup_psum.tile([P, 2, P, PACK], BF16, name="regroup_bank", tag="regroup_bank")
+                    regroup_banks[(block, g, half)] = bank
+                    for part in range(2):
+                        first = (2 * half + part) * P
+                        nc.tensor.matmul(
+                            out=bank[:, part].rearrange("p n t -> p (n t)"),
+                            lhsT=identity_bf16[:],
+                            rhs=w_raw[(block, g)][:, :, first:first + P].rearrange("p t n -> p n t"),
+                            start=True,
+                            stop=True,
+                        )
+
         def regroup(block):
             for g in range(PASSES):
                 if g % WIDE_QUANTISE == 0:
                     w_grouped[(block, g // WIDE_QUANTISE)] = grouped_pool.tile(
                         [P, WIDE_QUANTISE, WIDTH, PACK], BF16, name="w_grouped", tag="grouped", align_bytes=64)
                 target = w_grouped[(block, g // WIDE_QUANTISE)][:, g % WIDE_QUANTISE]
+                if g in TENSOR_CHUNKS[block]:
+                    for half in range(2):
+                        nc.scalar.copy(out=target[:, half * 2 * P:(half + 1) * 2 * P, :].rearrange("p n t -> p (n t)"),
+                                       in_=regroup_banks[(block, g, half)][:].rearrange("p a n t -> p (a n t)"))
+                    continue
                 target = target.rearrange("p (c i) t -> p c t i", i=4)
                 source = w_raw[(block, g)].rearrange("p t (c i) -> p c t i", i=4)
                 if g in VECTOR_CHUNKS[block]:
@@ -230,6 +256,7 @@ def tile_gqa_pa_kernel(tc, x, cos, sin, Wq, Wkv, out_0, out_1, out_2):
         store(0)
         quantise(1)
         for block in range(1, VALUE_BLOCK):
+            regroup_on_tensor(block + 1)
             regroup(block + 1)
             quantise(block + 1)
             multiply(block)
@@ -241,6 +268,7 @@ def tile_gqa_pa_kernel(tc, x, cos, sin, Wq, Wkv, out_0, out_1, out_2):
             if block < VALUE_BLOCK - 1:
                 rotate_add(block, 3)
                 store(block)
+        regroup_on_tensor(KEY_BLOCK)
         regroup(KEY_BLOCK)
         quantise(KEY_BLOCK)
         rotate_add(VALUE_BLOCK - 1, 3)

@@ -131,14 +131,13 @@ def tile_gqa_pa_kernel(tc, x, cos, sin, Wq, Wkv, out_0, out_1, out_2):
         def regroup_on_tensor(block):
             for g in TENSOR_CHUNKS[block]:
                 for half in range(2):
-                    bank = regroup_psum.tile([P, 2, P, PACK], BF16, name="regroup_bank", tag="regroup_bank")
+                    bank = regroup_psum.tile([P, 2 * P, PACK], BF16, name="regroup_bank", tag="regroup_bank")
                     regroup_banks[(block, g, half)] = bank
-                    for part in range(2):
-                        first = (2 * half + part) * P
+                    for pair in range(2):
                         nc.tensor.matmul(
-                            out=bank[:, part].rearrange("p n t -> p (n t)"),
+                            out=bank[:, :, 2 * pair:2 * pair + 2].rearrange("p n t -> p t n"),
                             lhsT=identity_bf16[:],
-                            rhs=w_raw[(block, g)][:, :, first:first + P].rearrange("p t n -> p n t"),
+                            rhs=w_raw[(block, g)][:, 2 * pair:2 * pair + 2, half * 2 * P:(half + 1) * 2 * P],
                             start=True,
                             stop=True,
                         )
@@ -152,7 +151,7 @@ def tile_gqa_pa_kernel(tc, x, cos, sin, Wq, Wkv, out_0, out_1, out_2):
                 if g in TENSOR_CHUNKS[block]:
                     for half in range(2):
                         nc.scalar.copy(out=target[:, half * 2 * P:(half + 1) * 2 * P, :].rearrange("p n t -> p (n t)"),
-                                       in_=regroup_banks[(block, g, half)][:].rearrange("p a n t -> p (a n t)"))
+                                       in_=regroup_banks[(block, g, half)][:].rearrange("p n t -> p (n t)"))
                     continue
                 target = target.rearrange("p (c i) t -> p c t i", i=4)
                 source = w_raw[(block, g)].rearrange("p t (c i) -> p c t i", i=4)

@@ -97,18 +97,20 @@ def tile_gqa_pa_kernel(tc, x, cos, sin, Wq, Wkv, out_0, out_1, out_2):
             load_block(block)
 
         table = const.tile([P, TILES, 2, PAIRS, 2], BF16, name="table")
-        nc.vector.tensor_copy(out=table[:, :, 0, :, 0], in_=cos_sb[:])
-        nc.vector.tensor_copy(out=table[:, :, 0, :, 1], in_=sin_sb[:])
-        nc.vector.tensor_scalar(out=table[:, :, 1, :, 0], in0=sin_sb[:],
-                                scalar1=-1.0, scalar2=0.0, op0=MULT, op1=ADD)
-        nc.vector.tensor_copy(out=table[:, :, 1, :, 1], in_=cos_sb[:])
+
+        def fill_table():
+            nc.vector.tensor_copy(out=table[:, :, 0, :, 0], in_=cos_sb[:])
+            nc.vector.tensor_copy(out=table[:, :, 0, :, 1], in_=sin_sb[:])
+            nc.vector.tensor_scalar(out=table[:, :, 1, :, 0], in0=sin_sb[:],
+                                    scalar1=-1.0, scalar2=0.0, op0=MULT, op1=ADD)
+            nc.vector.tensor_copy(out=table[:, :, 1, :, 1], in_=cos_sb[:])
 
         x_grouped = const.tile([P, TILES, PASSES, P, PACK], BF16, name="x_grouped", align_bytes=64)
         x_grouped_words = x_grouped[:].bitcast(F32)
         x_codes = const.tile([P, TILES, PASSES, P], U32, name="x_codes", align_bytes=64)
         x_scales = const.tile([P, TILES, PASSES, P], U8, name="x_scales", align_bytes=64)
 
-        def prepare_x(m):
+        def transpose_x(m):
             words = x_raw[m][:].bitcast(F32).rearrange("s (g p u) -> s g u p", g=PASSES, u=2)
             for half in range(2):
                 bank = psum.tile([P, 2, 2, P], F32, name="x_bank", tag="bank")
@@ -117,6 +119,8 @@ def tile_gqa_pa_kernel(tc, x, cos, sin, Wq, Wkv, out_0, out_1, out_2):
                         nc.tensor.transpose(bank[:, g, u, :], words[:, 2 * half + g, u, :], identity[:])
                 nc.scalar.copy(out=x_grouped_words[:, m, 2 * half:2 * half + 2, :, :],
                                in_=bank[:].rearrange("p g u s -> p g s u"))
+
+        def quantise_x(m):
             nc.vector.quantize_mx(
                 out=x_codes[:, m].rearrange("p g s -> p (g s)").bitcast(FP8X4),
                 scales=x_scales[:, m].rearrange("p g s -> p (g s)"),
@@ -142,8 +146,8 @@ def tile_gqa_pa_kernel(tc, x, cos, sin, Wq, Wkv, out_0, out_1, out_2):
                             stop=True,
                         )
 
-        def regroup(block):
-            for g in range(PASSES):
+        def regroup(block, passes=range(PASSES)):
+            for g in passes:
                 if g % WIDE_QUANTISE == 0:
                     w_grouped[(block, g // WIDE_QUANTISE)] = grouped_pool.tile(
                         [P, WIDE_QUANTISE, WIDTH, PACK], BF16, name="w_grouped", tag="grouped", align_bytes=64)
@@ -237,19 +241,21 @@ def tile_gqa_pa_kernel(tc, x, cos, sin, Wq, Wkv, out_0, out_1, out_2):
                 nc.scalar.copy(out=results[VALUE_BLOCK][:, :, m, :],
                                in_=sums[(VALUE_BLOCK, m)][:].rearrange("p (h l) -> p h l", h=HEADS))
 
-        prepare_x(0)
-        regroup(0)
+        transpose_x(0)
+        regroup(0, (0, 1))
+        quantise_x(0)
+        fill_table()
+        regroup(0, (2, 3))
         quantise(0)
         for m in range(1, TILES):
-            prepare_x(m)
+            transpose_x(m)
+            quantise_x(m)
         multiply(0)
-        rotate_multiply(0, 0)
-        rotate_add(0, 0)
-        rotate_multiply(0, 1)
-        rotate_add(0, 1)
         regroup(1)
-        rotate_multiply(0, 2)
-        rotate_multiply(0, 3)
+        for m in range(TILES):
+            rotate_multiply(0, m)
+            if m in GPSIMD_ADDS:
+                rotate_add(0, m)
         rotate_add(0, 2)
         rotate_add(0, 3)
         store(0)

@@ -25,8 +25,8 @@ PAIRS = 64
 VALUE_BLOCK = 4
 KEY_BLOCK = 5
 
-VECTOR_CHUNKS = ((0, 2, 3), (0, 2), (), (), (), ())
-TENSOR_CHUNKS = ((), (), (3,), (3,), (3,), (3,))
+VECTOR_CHUNKS = ((0, 2, 3), (0, 2), (2,), (), (), ())
+TENSOR_CHUNKS = ((), (), (), (), (3,), (3,))
 
 GPSIMD_ADDS = (0, 1)
 
@@ -57,8 +57,6 @@ def tile_gqa_pa_kernel(tc, x, cos, sin, Wq, Wkv, out_0, out_1, out_2):
 
         cos_sb = const.tile([P, TILES, PAIRS], BF16, name="cos_sb")
         sin_sb = const.tile([P, TILES, PAIRS], BF16, name="sin_sb")
-        nc.scalar.dma_start(out=cos_sb[:], in_=cos.rearrange("(p m) i -> p m i", m=TILES))
-        nc.scalar.dma_start(out=sin_sb[:], in_=sin.rearrange("(p m) i -> p m i", m=TILES))
         identity = const.tile([P, P], F32, name="identity")
         make_identity(nc, identity[:])
         identity_bf16 = const.tile([P, P], BF16, name="identity_bf16")
@@ -93,6 +91,8 @@ def tile_gqa_pa_kernel(tc, x, cos, sin, Wq, Wkv, out_0, out_1, out_2):
         load_block(0)
         for m in range(1, TILES):
             load_x(m)
+        nc.sync.dma_start(out=cos_sb[:], in_=cos.rearrange("(p m) i -> p m i", m=TILES))
+        nc.sync.dma_start(out=sin_sb[:], in_=sin.rearrange("(p m) i -> p m i", m=TILES))
         for block in range(1, BLOCKS):
             load_block(block)
 
@@ -235,6 +235,10 @@ def tile_gqa_pa_kernel(tc, x, cos, sin, Wq, Wkv, out_0, out_1, out_2):
         def store_tile(block, m):
             nc.sync.dma_start(out=out_view(block)[:, :, m * LANES:(m + 1) * LANES], in_=results[block][:, :, m, :])
 
+        def store_two_tiles(block, m):
+            nc.sync.dma_start(out=out_view(block)[:, :, m * LANES:(m + 2) * LANES],
+                              in_=results[block][:, :, m:m + 2, :].rearrange("p h m l -> p h (m l)"))
+
         def copy_values():
             results[VALUE_BLOCK] = result_pool.tile([P, HEADS, TILES, LANES], F32, name="result", tag="result")
             for m in range(TILES):
@@ -244,12 +248,13 @@ def tile_gqa_pa_kernel(tc, x, cos, sin, Wq, Wkv, out_0, out_1, out_2):
         transpose_x(0)
         regroup(0, (0, 1))
         quantise_x(0)
-        fill_table()
         regroup(0, (2, 3))
         quantise(0)
         for m in range(1, TILES):
             transpose_x(m)
             quantise_x(m)
+            if m == 1:
+                fill_table()
         multiply(0)
         regroup(1)
         for m in range(TILES):
@@ -273,11 +278,13 @@ def tile_gqa_pa_kernel(tc, x, cos, sin, Wq, Wkv, out_0, out_1, out_2):
             if block < VALUE_BLOCK - 1:
                 rotate_add(block, 3)
                 store(block)
+            else:
+                store_two_tiles(block, 0)
         regroup_on_tensor(KEY_BLOCK)
         regroup(KEY_BLOCK)
         quantise(KEY_BLOCK)
         rotate_add(VALUE_BLOCK - 1, 3)
-        store(VALUE_BLOCK - 1)
+        store_two_tiles(VALUE_BLOCK - 1, 2)
         multiply(VALUE_BLOCK)
         copy_values()
         store(VALUE_BLOCK)

@@ -25,7 +25,7 @@ PAIRS = 64
 VALUE_BLOCK = 4
 KEY_BLOCK = 5
 
-VECTOR_CHUNKS = ((0, 2, 3), (0, 2), (2,), (), (), ())
+VECTOR_CHUNKS = ((0, 2, 3), (2, 3), (2,), (), (), ())
 TENSOR_CHUNKS = ((), (), (), (), (3,), (3,))
 
 GPSIMD_ADDS = (0, 1)
@@ -42,7 +42,7 @@ def tile_gqa_pa_kernel(tc, x, cos, sin, Wq, Wkv, out_0, out_1, out_2):
         raw_kv_pool = ctx.enter_context(tc.tile_pool(name="raw_kv", bufs=PASSES))
         grouped_pool = ctx.enter_context(tc.tile_pool(name="grouped", bufs=REGROUP_AHEAD * PASSES // WIDE_QUANTISE))
         code_pool = ctx.enter_context(tc.tile_pool(name="codes", bufs=3))
-        product_pool = ctx.enter_context(tc.tile_pool(name="products", bufs=4))
+        product_pool = ctx.enter_context(tc.tile_pool(name="products", bufs=2))
         result_pool = ctx.enter_context(tc.tile_pool(name="results", bufs=3))
         psum = ctx.enter_context(tc.psum_pool(name="psum", bufs=6))
         regroup_psum = ctx.enter_context(tc.psum_pool(name="regroup_psum", bufs=2))
@@ -203,17 +203,25 @@ def tile_gqa_pa_kernel(tc, x, cos, sin, Wq, Wkv, out_0, out_1, out_2):
                 sums[(block, m)] = psum.tile([P, WIDTH], F32, name="sums", tag="bank")
                 for g in range(PASSES):
                     one_pass(block, m, g)
+                if m == 0 and 0 < block < KEY_BLOCK:
+                    regroup_on_tensor(block + 1)
 
         results = {}
         products_of = {}
+        late_products = {}
 
         def rotate_multiply(block, m):
             if block not in results:
                 results[block] = result_pool.tile([P, HEADS, TILES, LANES], F32, name="result", tag="result")
-            products = product_pool.tile([P, 2, HEADS, PAIRS, 2], F32, name="products", tag="products")
-            products_of[(block, m)] = products
+            if m in GPSIMD_ADDS:
+                products = product_pool.tile([P, 2, HEADS, PAIRS, 2], F32, name="products", tag="products")
+                products_of[(block, m)] = products[:]
+            else:
+                if m == 2:
+                    late_products[block] = product_pool.tile([P, 2, 2, HEADS, PAIRS, 2], F32, name="late_products", tag="late_products")
+                products_of[(block, m)] = late_products[block][:, m - 2]
             nc.vector.tensor_tensor(
-                out=products[:],
+                out=products_of[(block, m)],
                 in0=sums[(block, m)][:].rearrange("p (h i q) -> p q h i", h=HEADS, q=2).unsqueeze(4).to_broadcast([P, 2, HEADS, PAIRS, 2]),
                 in1=table[:, m].unsqueeze(2).to_broadcast([P, 2, HEADS, PAIRS, 2]),
                 op=MULT,
@@ -226,6 +234,15 @@ def tile_gqa_pa_kernel(tc, x, cos, sin, Wq, Wkv, out_0, out_1, out_2):
                 out=results[block][:, :, m, :],
                 in0=products[:, 0].rearrange("p h i y -> p h (i y)"),
                 in1=products[:, 1].rearrange("p h i y -> p h (i y)"),
+                op=ADD,
+            )
+
+        def rotate_add_late(block):
+            products = late_products[block]
+            nc.vector.tensor_tensor(
+                out=results[block][:, :, 2:4, :].rearrange("p h m l -> p m h l"),
+                in0=products[:, :, 0].rearrange("p m h i y -> p m h (i y)"),
+                in1=products[:, :, 1].rearrange("p m h i y -> p m h (i y)"),
                 op=ADD,
             )
 
@@ -256,36 +273,32 @@ def tile_gqa_pa_kernel(tc, x, cos, sin, Wq, Wkv, out_0, out_1, out_2):
             if m == 1:
                 fill_table()
         multiply(0)
-        regroup(1)
         for m in range(TILES):
             rotate_multiply(0, m)
             if m in GPSIMD_ADDS:
                 rotate_add(0, m)
-        rotate_add(0, 2)
-        rotate_add(0, 3)
+        rotate_add_late(0)
         store(0)
+        regroup(1)
         quantise(1)
         for block in range(1, VALUE_BLOCK):
-            regroup_on_tensor(block + 1)
+            multiply(block)
             regroup(block + 1)
             quantise(block + 1)
-            multiply(block)
             for m in range(TILES):
                 rotate_multiply(block, m)
                 if m in GPSIMD_ADDS:
                     rotate_add(block, m)
-            rotate_add(block, 2)
             if block < VALUE_BLOCK - 1:
-                rotate_add(block, 3)
+                rotate_add_late(block)
                 store(block)
             else:
                 store_two_tiles(block, 0)
-        regroup_on_tensor(KEY_BLOCK)
+        multiply(VALUE_BLOCK)
         regroup(KEY_BLOCK)
         quantise(KEY_BLOCK)
-        rotate_add(VALUE_BLOCK - 1, 3)
+        rotate_add_late(VALUE_BLOCK - 1)
         store_two_tiles(VALUE_BLOCK - 1, 2)
-        multiply(VALUE_BLOCK)
         copy_values()
         store(VALUE_BLOCK)
         multiply(KEY_BLOCK)

@@ -26,7 +26,7 @@ VALUE_BLOCK = 4
 KEY_BLOCK = 5
 
 VECTOR_CHUNKS = ((0, 2, 3), (2, 3), (2,), (), (), ())
-TENSOR_CHUNKS = ((), (), (), (), (3,), (3,))
+TENSOR_CHUNKS = ((), (), (), (3,), (3,), (3,))
 
 GPSIMD_ADDS = (0, 1)
 
@@ -42,7 +42,7 @@ def tile_gqa_pa_kernel(tc, x, cos, sin, Wq, Wkv, out_0, out_1, out_2):
         raw_kv_pool = ctx.enter_context(tc.tile_pool(name="raw_kv", bufs=PASSES))
         grouped_pool = ctx.enter_context(tc.tile_pool(name="grouped", bufs=REGROUP_AHEAD * PASSES // WIDE_QUANTISE))
         code_pool = ctx.enter_context(tc.tile_pool(name="codes", bufs=3))
-        product_pool = ctx.enter_context(tc.tile_pool(name="products", bufs=2))
+        product_pool = ctx.enter_context(tc.tile_pool(name="products", bufs=4))
         result_pool = ctx.enter_context(tc.tile_pool(name="results", bufs=3))
         psum = ctx.enter_context(tc.psum_pool(name="psum", bufs=6))
         regroup_psum = ctx.enter_context(tc.psum_pool(name="regroup_psum", bufs=2))
@@ -208,20 +208,14 @@ def tile_gqa_pa_kernel(tc, x, cos, sin, Wq, Wkv, out_0, out_1, out_2):
 
         results = {}
         products_of = {}
-        late_products = {}
 
         def rotate_multiply(block, m):
             if block not in results:
                 results[block] = result_pool.tile([P, HEADS, TILES, LANES], F32, name="result", tag="result")
-            if m in GPSIMD_ADDS:
-                products = product_pool.tile([P, 2, HEADS, PAIRS, 2], F32, name="products", tag="products")
-                products_of[(block, m)] = products[:]
-            else:
-                if m == 2:
-                    late_products[block] = product_pool.tile([P, 2, 2, HEADS, PAIRS, 2], F32, name="late_products", tag="late_products")
-                products_of[(block, m)] = late_products[block][:, m - 2]
+            products = product_pool.tile([P, 2, HEADS, PAIRS, 2], F32, name="products", tag="products")
+            products_of[(block, m)] = products
             nc.vector.tensor_tensor(
-                out=products_of[(block, m)],
+                out=products[:],
                 in0=sums[(block, m)][:].rearrange("p (h i q) -> p q h i", h=HEADS, q=2).unsqueeze(4).to_broadcast([P, 2, HEADS, PAIRS, 2]),
                 in1=table[:, m].unsqueeze(2).to_broadcast([P, 2, HEADS, PAIRS, 2]),
                 op=MULT,
@@ -238,13 +232,9 @@ def tile_gqa_pa_kernel(tc, x, cos, sin, Wq, Wkv, out_0, out_1, out_2):
             )
 
         def rotate_add_late(block):
-            products = late_products[block]
-            nc.vector.tensor_tensor(
-                out=results[block][:, :, 2:4, :].rearrange("p h m l -> p m h l"),
-                in0=products[:, :, 0].rearrange("p m h i y -> p m h (i y)"),
-                in1=products[:, :, 1].rearrange("p m h i y -> p m h (i y)"),
-                op=ADD,
-            )
+            for m in range(TILES):
+                if m not in GPSIMD_ADDS:
+                    rotate_add(block, m)
 
         def store(block):
             nc.sync.dma_start(out=out_view(block), in_=results[block][:].rearrange("p h m l -> p h (m l)"))
@@ -277,10 +267,10 @@ def tile_gqa_pa_kernel(tc, x, cos, sin, Wq, Wkv, out_0, out_1, out_2):
             rotate_multiply(0, m)
             if m in GPSIMD_ADDS:
                 rotate_add(0, m)
-        rotate_add_late(0)
-        store(0)
         regroup(1)
         quantise(1)
+        rotate_add_late(0)
+        store(0)
         for block in range(1, VALUE_BLOCK):
             multiply(block)
             regroup(block + 1)

@@ -221,13 +221,13 @@ def tile_gqa_pa_kernel(tc, x, cos, sin, Wq, Wkv, out_0, out_1, out_2):
                 op=MULT,
             )
 
-        def rotate_add(block, m):
+        def rotate_add(block, m, heads=slice(0, HEADS)):
             engine = nc.gpsimd if m in GPSIMD_ADDS else nc.vector
             products = products_of[(block, m)]
             engine.tensor_tensor(
-                out=results[block][:, :, m, :],
-                in0=products[:, 0].rearrange("p h i y -> p h (i y)"),
-                in1=products[:, 1].rearrange("p h i y -> p h (i y)"),
+                out=results[block][:, heads, m, :],
+                in0=products[:, 0, heads].rearrange("p h i y -> p h (i y)"),
+                in1=products[:, 1, heads].rearrange("p h i y -> p h (i y)"),
                 op=ADD,
             )
 
@@ -239,8 +239,8 @@ def tile_gqa_pa_kernel(tc, x, cos, sin, Wq, Wkv, out_0, out_1, out_2):
         def store(block):
             nc.sync.dma_start(out=out_view(block), in_=results[block][:].rearrange("p h m l -> p h (m l)"))
 
-        def store_tile(block, m):
-            nc.sync.dma_start(out=out_view(block)[:, :, m * LANES:(m + 1) * LANES], in_=results[block][:, :, m, :])
+        def store_tile(block, m, heads=slice(0, HEADS)):
+            nc.sync.dma_start(out=out_view(block)[:, heads, m * LANES:(m + 1) * LANES], in_=results[block][:, heads, m, :])
 
         def store_two_tiles(block, m):
             nc.sync.dma_start(out=out_view(block)[:, :, m * LANES:(m + 2) * LANES],
@@ -287,8 +287,10 @@ def tile_gqa_pa_kernel(tc, x, cos, sin, Wq, Wkv, out_0, out_1, out_2):
         multiply(VALUE_BLOCK)
         regroup(KEY_BLOCK)
         quantise(KEY_BLOCK)
-        rotate_add_late(VALUE_BLOCK - 1)
-        store_two_tiles(VALUE_BLOCK - 1, 2)
+        for m in range(TILES):
+            if m not in GPSIMD_ADDS:
+                rotate_add(VALUE_BLOCK - 1, m)
+                store_tile(VALUE_BLOCK - 1, m)
         copy_values()
         store(VALUE_BLOCK)
         multiply(KEY_BLOCK)
@@ -297,7 +299,8 @@ def tile_gqa_pa_kernel(tc, x, cos, sin, Wq, Wkv, out_0, out_1, out_2):
             if m in GPSIMD_ADDS:
                 rotate_add(KEY_BLOCK, m)
                 store_tile(KEY_BLOCK, m)
-        for m in range(TILES):
-            if m not in GPSIMD_ADDS:
-                rotate_add(KEY_BLOCK, m)
-                store_tile(KEY_BLOCK, m)
+        rotate_add(KEY_BLOCK, 2)
+        store_tile(KEY_BLOCK, 2)
+        for heads in (slice(0, HEADS // 2), slice(HEADS // 2, HEADS)):
+            rotate_add(KEY_BLOCK, 3, heads)
+            store_tile(KEY_BLOCK, 3, heads)

from contextlib import ExitStack

import concourse.mybir as mybir
from concourse.masks import make_identity

FLOPS = 2 * 512 * 2048 * 3072

BF16 = mybir.dt.bfloat16
F32 = mybir.dt.float32
U32 = mybir.dt.uint32
U8 = mybir.dt.uint8
FP8X4 = mybir.dt.float8_e4m3fn_x4
MULT = mybir.AluOpType.mult
ADD = mybir.AluOpType.add

P = 128
PACK = 4
TILES = 4
PASSES = 4
BLOCKS = 6
WIDTH = 512
HEADS = 4
LANES = 128
PAIRS = 64
VALUE_BLOCK = 4
KEY_BLOCK = 5

VECTOR_CHUNKS = ((0, 2, 3), (2, 3), (2,), (), (), ())
TENSOR_CHUNKS = ((), (), (), (3,), (3,), (3,))

GPSIMD_ADDS = (0, 1)

REGROUP_AHEAD = 2
WIDE_QUANTISE = 2


def tile_gqa_pa_kernel(tc, x, cos, sin, Wq, Wkv, out_0, out_1, out_2):
    nc = tc.nc
    with ExitStack() as ctx:
        const = ctx.enter_context(tc.tile_pool(name="const", bufs=1))
        raw_pool = ctx.enter_context(tc.tile_pool(name="raw", bufs=TILES + 3 * PASSES))
        raw_kv_pool = ctx.enter_context(tc.tile_pool(name="raw_kv", bufs=PASSES))
        grouped_pool = ctx.enter_context(tc.tile_pool(name="grouped", bufs=REGROUP_AHEAD * PASSES // WIDE_QUANTISE))
        code_pool = ctx.enter_context(tc.tile_pool(name="codes", bufs=3))
        product_pool = ctx.enter_context(tc.tile_pool(name="products", bufs=4))
        result_pool = ctx.enter_context(tc.tile_pool(name="results", bufs=3))
        psum = ctx.enter_context(tc.psum_pool(name="psum", bufs=6))
        regroup_psum = ctx.enter_context(tc.psum_pool(name="regroup_psum", bufs=2))

        x_view = x.rearrange("b (p m) k -> p (b m) k", m=TILES)
        out_views = [o.rearrange("b h (p m) l -> p (b h) (m l)", m=TILES) for o in (out_0, out_1, out_2)]

        def out_view(block):
            if block < 4:
                return out_views[0][:, block * HEADS:(block + 1) * HEADS, :]
            return out_views[1 if block == KEY_BLOCK else 2][:, :, :]

        cos_sb = const.tile([P, TILES, PAIRS], BF16, name="cos_sb")
        sin_sb = const.tile([P, TILES, PAIRS], BF16, name="sin_sb")
        identity = const.tile([P, P], F32, name="identity")
        make_identity(nc, identity[:])
        identity_bf16 = const.tile([P, P], BF16, name="identity_bf16")
        make_identity(nc, identity_bf16[:])
        ctx.enter_context(tc.manual_schedule())

        x_raw = {}
        w_raw = {}

        def load_x(m):
            x_raw[m] = raw_pool.tile([P, PASSES * WIDTH], BF16, name="x_raw", tag="raw")
            nc.sync.dma_start(out=x_raw[m][:], in_=x_view[:, m, :])

        def load_block(block):
            if block == KEY_BLOCK:
                return
            for g in range(PASSES):
                if block == VALUE_BLOCK:
                    both = raw_kv_pool.tile([P, PACK, 2 * WIDTH], BF16, name="kv_raw", tag="raw_kv")
                    nc.sync.dma_start(out=both[:], in_=Wkv[g * 512:(g + 1) * 512, :].rearrange("(p t) n -> p t n", t=PACK))
                    w_raw[(KEY_BLOCK, g)] = both[:, :, 0:WIDTH]
                    w_raw[(VALUE_BLOCK, g)] = both[:, :, WIDTH:2 * WIDTH]
                    continue
                chunk = raw_pool.tile([P, PACK, WIDTH], BF16, name="w_raw", tag="raw")
                nc.sync.dma_start(
                    out=chunk[:],
                    in_=Wq[g * 512:(g + 1) * 512, block * WIDTH:(block + 1) * WIDTH].rearrange("(p t) n -> p t n", t=PACK),
                )
                w_raw[(block, g)] = chunk[:]

        load_x(0)
        load_block(0)
        for m in range(1, TILES):
            load_x(m)
        nc.sync.dma_start(out=cos_sb[:], in_=cos.rearrange("(p m) i -> p m i", m=TILES))
        nc.sync.dma_start(out=sin_sb[:], in_=sin.rearrange("(p m) i -> p m i", m=TILES))
        for block in range(1, BLOCKS):
            load_block(block)

        table = const.tile([P, TILES, 2, PAIRS, 2], BF16, name="table")

        def fill_table():
            nc.vector.tensor_copy(out=table[:, :, 0, :, 0], in_=cos_sb[:])
            nc.vector.tensor_copy(out=table[:, :, 0, :, 1], in_=sin_sb[:])
            nc.vector.tensor_scalar(out=table[:, :, 1, :, 0], in0=sin_sb[:],
                                    scalar1=-1.0, scalar2=0.0, op0=MULT, op1=ADD)
            nc.vector.tensor_copy(out=table[:, :, 1, :, 1], in_=cos_sb[:])

        x_grouped = const.tile([P, TILES, PASSES, P, PACK], BF16, name="x_grouped", align_bytes=64)
        x_grouped_words = x_grouped[:].bitcast(F32)
        x_codes = const.tile([P, TILES, PASSES, P], U32, name="x_codes", align_bytes=64)
        x_scales = const.tile([P, TILES, PASSES, P], U8, name="x_scales", align_bytes=64)

        def transpose_x(m):
            words = x_raw[m][:].bitcast(F32).rearrange("s (g p u) -> s g u p", g=PASSES, u=2)
            for half in range(2):
                bank = psum.tile([P, 2, 2, P], F32, name="x_bank", tag="bank")
                for g in range(2):
                    for u in range(2):
                        nc.tensor.transpose(bank[:, g, u, :], words[:, 2 * half + g, u, :], identity[:])
                nc.scalar.copy(out=x_grouped_words[:, m, 2 * half:2 * half + 2, :, :],
                               in_=bank[:].rearrange("p g u s -> p g s u"))

        def quantise_x(m):
            nc.vector.quantize_mx(
                out=x_codes[:, m].rearrange("p g s -> p (g s)").bitcast(FP8X4),
                scales=x_scales[:, m].rearrange("p g s -> p (g s)"),
                in_=x_grouped[:, m].rearrange("p g s t -> p (g s t)"),
            )

        w_grouped = {}
        w_codes = {}

        regroup_banks = {}

        def regroup_on_tensor(block):
            for g in TENSOR_CHUNKS[block]:
                for half in range(2):
                    bank = regroup_psum.tile([P, 2 * P, PACK], BF16, name="regroup_bank", tag="regroup_bank")
                    regroup_banks[(block, g, half)] = bank
                    for pair in range(2):
                        nc.tensor.matmul(
                            out=bank[:, :, 2 * pair:2 * pair + 2].rearrange("p n t -> p t n"),
                            lhsT=identity_bf16[:],
                            rhs=w_raw[(block, g)][:, 2 * pair:2 * pair + 2, half * 2 * P:(half + 1) * 2 * P],
                            start=True,
                            stop=True,
                        )

        def regroup(block, passes=range(PASSES)):
            for g in passes:
                if g % WIDE_QUANTISE == 0:
                    w_grouped[(block, g // WIDE_QUANTISE)] = grouped_pool.tile(
                        [P, WIDE_QUANTISE, WIDTH, PACK], BF16, name="w_grouped", tag="grouped", align_bytes=64)
                target = w_grouped[(block, g // WIDE_QUANTISE)][:, g % WIDE_QUANTISE]
                if g in TENSOR_CHUNKS[block]:
                    for half in range(2):
                        nc.scalar.copy(out=target[:, half * 2 * P:(half + 1) * 2 * P, :].rearrange("p n t -> p (n t)"),
                                       in_=regroup_banks[(block, g, half)][:].rearrange("p n t -> p (n t)"))
                    continue
                target = target.rearrange("p (c i) t -> p c t i", i=4)
                source = w_raw[(block, g)].rearrange("p t (c i) -> p c t i", i=4)
                if g in VECTOR_CHUNKS[block]:
                    nc.vector.tensor_copy(out=target, in_=source)
                else:
                    nc.scalar.copy(out=target, in_=source)

        def quantise(block):
            codes = code_pool.tile([P, PASSES, WIDTH], U32, name="codes", tag="codes", align_bytes=64)
            scales = code_pool.tile([P, PASSES, WIDTH], U8, name="scales", tag="scales", align_bytes=64)
            w_codes[block] = (codes, scales)
            for pair in range(PASSES // WIDE_QUANTISE):
                first = pair * WIDE_QUANTISE
                if block == BLOCKS - 1:
                    for j in range(WIDE_QUANTISE):
                        nc.vector.quantize_mx(
                            out=codes[:, first + j, :].bitcast(FP8X4),
                            scales=scales[:, first + j, :],
                            in_=w_grouped[(block, pair)][:, j].rearrange("p n t -> p (n t)"),
                        )
                    continue
                nc.vector.quantize_mx(
                    out=codes[:, first:first + WIDE_QUANTISE, :].rearrange("p g n -> p (g n)").bitcast(FP8X4),
                    scales=scales[:, first:first + WIDE_QUANTISE, :].rearrange("p g n -> p (g n)"),
                    in_=w_grouped[(block, pair)][:].rearrange("p g n t -> p (g n t)"),
                )

        sums = {}

        def one_pass(block, m, g):
            codes, scales = w_codes[block]
            nc.tensor.matmul_mx(
                out=sums[(block, m)][:],
                lhsT=x_codes[:, m, g, :].bitcast(FP8X4),
                lhsT_scale=x_scales[:, m, g, :],
                rhs=codes[:, g, :].bitcast(FP8X4),
                rhs_scale=scales[:, g, :],
                start=(g == 0),
                stop=(g == PASSES - 1),
            )

        def multiply(block):
            for m in range(TILES):
                sums[(block, m)] = psum.tile([P, WIDTH], F32, name="sums", tag="bank")
                for g in range(PASSES):
                    one_pass(block, m, g)
                if m == 0 and 0 < block < KEY_BLOCK:
                    regroup_on_tensor(block + 1)

        results = {}
        products_of = {}

        def rotate_multiply(block, m):
            if block not in results:
                results[block] = result_pool.tile([P, HEADS, TILES, LANES], F32, name="result", tag="result")
            products = product_pool.tile([P, 2, HEADS, PAIRS, 2], F32, name="products", tag="products")
            products_of[(block, m)] = products
            nc.vector.tensor_tensor(
                out=products[:],
                in0=sums[(block, m)][:].rearrange("p (h i q) -> p q h i", h=HEADS, q=2).unsqueeze(4).to_broadcast([P, 2, HEADS, PAIRS, 2]),
                in1=table[:, m].unsqueeze(2).to_broadcast([P, 2, HEADS, PAIRS, 2]),
                op=MULT,
            )

        def rotate_add(block, m, heads=slice(0, HEADS)):
            engine = nc.gpsimd if m in GPSIMD_ADDS else nc.vector
            products = products_of[(block, m)]
            engine.tensor_tensor(
                out=results[block][:, heads, m, :],
                in0=products[:, 0, heads].rearrange("p h i y -> p h (i y)"),
                in1=products[:, 1, heads].rearrange("p h i y -> p h (i y)"),
                op=ADD,
            )

        def rotate_add_late(block):
            for m in range(TILES):
                if m not in GPSIMD_ADDS:
                    rotate_add(block, m)

        def store(block):
            nc.sync.dma_start(out=out_view(block), in_=results[block][:].rearrange("p h m l -> p h (m l)"))

        def store_tile(block, m, heads=slice(0, HEADS)):
            nc.sync.dma_start(out=out_view(block)[:, heads, m * LANES:(m + 1) * LANES], in_=results[block][:, heads, m, :])

        def store_two_tiles(block, m):
            nc.sync.dma_start(out=out_view(block)[:, :, m * LANES:(m + 2) * LANES],
                              in_=results[block][:, :, m:m + 2, :].rearrange("p h m l -> p h (m l)"))

        def copy_values():
            results[VALUE_BLOCK] = result_pool.tile([P, HEADS, TILES, LANES], F32, name="result", tag="result")
            for m in range(TILES):
                nc.scalar.copy(out=results[VALUE_BLOCK][:, :, m, :],
                               in_=sums[(VALUE_BLOCK, m)][:].rearrange("p (h l) -> p h l", h=HEADS))

        transpose_x(0)
        regroup(0, (0, 1))
        quantise_x(0)
        regroup(0, (2, 3))
        quantise(0)
        for m in range(1, TILES):
            transpose_x(m)
            quantise_x(m)
            if m == 1:
                fill_table()
        multiply(0)
        for m in range(TILES):
            rotate_multiply(0, m)
            if m in GPSIMD_ADDS:
                rotate_add(0, m)
        regroup(1)
        quantise(1)
        rotate_add_late(0)
        store(0)
        for block in range(1, VALUE_BLOCK):
            multiply(block)
            regroup(block + 1)
            quantise(block + 1)
            for m in range(TILES):
                rotate_multiply(block, m)
                if m in GPSIMD_ADDS:
                    rotate_add(block, m)
            if block < VALUE_BLOCK - 1:
                rotate_add_late(block)
                store(block)
            else:
                store_two_tiles(block, 0)
        multiply(VALUE_BLOCK)
        regroup(KEY_BLOCK)
        quantise(KEY_BLOCK)
        for m in range(TILES):
            if m not in GPSIMD_ADDS:
                rotate_add(VALUE_BLOCK - 1, m)
                store_tile(VALUE_BLOCK - 1, m)
        copy_values()
        store(VALUE_BLOCK)
        multiply(KEY_BLOCK)
        for m in range(TILES):
            rotate_multiply(KEY_BLOCK, m)
            if m in GPSIMD_ADDS:
                rotate_add(KEY_BLOCK, m)
                store_tile(KEY_BLOCK, m)
        rotate_add(KEY_BLOCK, 2)
        store_tile(KEY_BLOCK, 2)
        for heads in (slice(0, HEADS // 2), slice(HEADS // 2, HEADS)):
            rotate_add(KEY_BLOCK, 3, heads)
            store_tile(KEY_BLOCK, 3, heads)
